import numpy as np
import ml_dtypes

BF16 = ml_dtypes.bfloat16


def bf(x):
    return np.asarray(x, np.float32).astype(BF16)


def f32(x):
    return np.asarray(x, np.float32)


def f64(x):
    return np.asarray(x).astype(np.float64)


def striped(idx):
    return np.tile(idx.reshape(-1, 16).T, (8, 1))


C, S, A, N, M, H = 256, 1024, 4, 4096, 128, 512
B2 = 0.25


def setup_inputs():
    return {"x": f32(np.random.standard_normal((C, S))), "dist": f32(np.random.uniform(0.0, 1.0, (1, N))), "w1": f32(np.random.standard_normal((M, 1))), "b1": f32(0.5 * np.random.standard_normal((M, 1))), "w2": bf((0.5 + np.random.standard_normal((M, 1))) * (8.0 / M)), "wh": bf(np.random.standard_normal((C + C, M)) / np.sqrt(C + C)), "bh": f32(0.1 * np.random.standard_normal((M, 1))), "offs": striped(np.concatenate([np.random.permutation(S)[:H] for _ in range(N // H)]))}


def reference(x, dist, w1, b1, w2, wh, bh, offs):
    idx = offs[:16].T.reshape(-1)
    hid = np.maximum(f64(w1) * f64(dist) + f64(b1), 0.0)
    d = f64(w2).T @ hid + B2
    msg = f64(x)[:, idx] * d
    own = np.repeat(f64(x), A, axis=1)
    h = np.maximum(f64(wh).T @ np.concatenate([msg, own], axis=0) + f64(bh), 0.0)
    return h.reshape(M, S, A).mean(axis=2)

@@ -1,0 +1,142 @@
+import concourse.mybir as mybir
+
+F32 = mybir.dt.float32
+BF16 = mybir.dt.bfloat16
+U16 = mybir.dt.uint16
+RELU = mybir.ActivationFunctionType.Relu
+COPY = mybir.ActivationFunctionType.Copy
+MULT = mybir.AluOpType.mult
+ADD = mybir.AluOpType.add
+
+P = 128
+C = 256
+S = 1024
+A = 4
+N = S * A
+M = 128
+BLOCKS = C // P
+PIECE = 512
+PIECES = N // PIECE
+NODES = PIECE // A
+AHEAD = 2
+
+FLOPS = 2 * M * C * N + 2 * M * C * S + 2 * M * N
+
+
+def tile_pgnn_layer_kernel(tc, x, dist, w1, b1, w2, wh, bh, offs, out):
+    nc = tc.nc
+    with (
+        tc.tile_pool(name="held", bufs=1) as held,
+        tc.tile_pool(name="work", bufs=3) as work,
+        tc.tile_pool(name="ahead", bufs=AHEAD + 2) as ahead,
+        tc.psum_pool(name="psum_d", bufs=2) as psum_d,
+        tc.psum_pool(name="psum_z", bufs=3) as psum_z,
+    ):
+        scratch = held.tile([P, 1], F32, name="scratch")
+        nc.vector.memset(scratch[:], 0.0)
+        nc.scalar.activation(scratch[:], scratch[:], RELU)
+
+        w1_col = held.tile([P, 1], F32, name="w1_col")
+        b1_col = held.tile([P, 1], F32, name="b1_col")
+        w2_col = held.tile([P, 1], BF16, name="w2_col")
+        bh_col = held.tile([P, 1], F32, name="bh_col")
+        wh_sb = held.tile([P, 2 * BLOCKS, M], BF16, name="wh_sb")
+        offsets = held.tile([P, N // 16], U16, name="offsets")
+        x_f32 = [held.tile([P, S], F32, name=f"x_f32_{b}") for b in range(BLOCKS)]
+        dist_row = dist.rearrange("o n -> (o n)")
+        dist_all = [held.tile([P, PIECE], F32, name=f"dist_all{k}") for k in range(PIECES)]
+
+        def load_dist(k):
+            nc.sync.dma_start(
+                dist_all[k][:], dist_row[k * PIECE : (k + 1) * PIECE].partition_broadcast(P)
+            )
+
+        with nc.allow_non_contiguous_dma(reason="one element to a partition"):
+            nc.sync.dma_start(w1_col[:], w1)
+            nc.sync.dma_start(b1_col[:], b1)
+            load_dist(0)
+            nc.sync.dma_start(w2_col[:], w2)
+        nc.sync.dma_start(offsets[:], offs)
+        for b in range(BLOCKS):
+            nc.sync.dma_start(x_f32[b][:], x[b * P : (b + 1) * P, :])
+        load_dist(1)
+        nc.sync.dma_start(wh_sb[:], wh.rearrange("(k p) m -> p k m", p=P))
+        with nc.allow_non_contiguous_dma(reason="one element to a partition"):
+            nc.sync.dma_start(bh_col[:], bh)
+        for k in range(2, PIECES):
+            load_dist(k)
+
+        w2_wide = held.tile([P, M], BF16, name="w2_wide")
+        nc.vector.tensor_copy(w2_wide[:], w2_col[:, 0:1].to_broadcast([P, M]))
+        bh_quarter = held.tile([P, 1], F32, name="bh_quarter")
+        nc.gpsimd.tensor_scalar_mul(bh_quarter[:], bh_col[:], 0.25)
+
+        x_bf = [held.tile([P, S], BF16, name=f"x_bf_{b}") for b in range(BLOCKS)]
+
+        def cast(b, dst, src):
+            if b == 0:
+                nc.gpsimd.tensor_copy(dst, src)
+            else:
+                nc.scalar.activation(dst, src, COPY)
+
+        d_ps = {}
+        d_sb = {}
+
+        def start_d(k):
+            hid = work.tile([P, PIECE], BF16, name="hid")
+            nc.scalar.activation(
+                hid[:], dist_all[k][:], RELU, bias=b1_col[:, 0:1], scale=w1_col[:, 0:1]
+            )
+            d_ps[k] = psum_d.tile([P, PIECE], F32, name="d_ps")
+            nc.tensor.matmul(d_ps[k][:], w2_wide[:], hid[:], start=True, stop=True)
+
+        def finish_d(k):
+            d_sb[k] = ahead.tile([P, PIECE], F32, name="d_sb")
+            nc.scalar.activation(d_sb[k][:], d_ps[k][:], COPY, bias=0.25)
+
+        start_d(0)
+        for k in range(AHEAD):
+            start_d(k + 1)
+            finish_d(k)
+        for b in range(BLOCKS):
+            cast(b, x_bf[b][:], x_f32[b][:])
+
+        for k in range(PIECES):
+            if k + AHEAD + 1 < PIECES:
+                start_d(k + AHEAD + 1)
+            if k + AHEAD < PIECES:
+                finish_d(k + AHEAD)
+
+            z_ps = psum_z.tile([P, PIECE], F32, name="z_ps")
+            z_by_node = z_ps[:].rearrange("p (n a) -> p n a", a=A)
+            for b in range(BLOCKS):
+                own = x_bf[b][:, k * NODES : (k + 1) * NODES]
+                nc.tensor.matmul(
+                    z_by_node,
+                    wh_sb[:, BLOCKS + b, :],
+                    own.unsqueeze(2).to_broadcast([P, NODES, A]),
+                    start=(b == 0),
+                    stop=False,
+                )
+            for b in range(BLOCKS):
+                msg = work.tile([P, PIECE], F32, name=f"msg{b}")
+                nc.vector.tensor_tensor(
+                    msg[:],
+                    x_f32[b][:].indirect(offsets[:, k * (PIECE // 16) : (k + 1) * (PIECE // 16)]),
+                    d_sb[k][:],
+                    MULT,
+                )
+                msg_bf = work.tile([P, PIECE], BF16, name=f"msg_bf{b}")
+                cast(b, msg_bf[:], msg[:])
+                nc.tensor.matmul(
+                    z_ps[:], wh_sb[:, b, :], msg_bf[:], start=False, stop=(b == BLOCKS - 1)
+                )
+
+            h = work.tile([P, PIECE], F32, name="h")
+            nc.scalar.activation(h[:], z_ps[:], RELU, bias=bh_quarter[:, 0:1], scale=0.25)
+            h_by_node = h[:].rearrange("p (n a) -> p n a", a=A)
+            pair = work.tile([P, NODES, 2], F32, name="pair")
+            nc.gpsimd.tensor_tensor(pair[:], h_by_node[:, :, 0:2], h_by_node[:, :, 2:4], ADD)
+            mean = work.tile([P, NODES], F32, name="mean")
+            nc.gpsimd.tensor_tensor(mean[:], pair[:, :, 0], pair[:, :, 1], ADD)
+            nc.sync.dma_start(out[:, k * NODES : (k + 1) * NODES], mean[:])

@@ -1,4 +1,5 @@
 import concourse.mybir as mybir
+from concourse.masks import make_identity
 
 F32 = mybir.dt.float32
 BF16 = mybir.dt.bfloat16
@@ -6,7 +7,6 @@ U16 = mybir.dt.uint16
 RELU = mybir.ActivationFunctionType.Relu
 COPY = mybir.ActivationFunctionType.Copy
 MULT = mybir.AluOpType.mult
-ADD = mybir.AluOpType.add
 
 P = 128
 C = 256
@@ -31,6 +31,7 @@ def tile_pgnn_layer_kernel(tc, x, dist, w1, b1, w2, wh, bh, offs, out):
         tc.tile_pool(name="ahead", bufs=AHEAD + 2) as ahead,
         tc.psum_pool(name="psum_d", bufs=2) as psum_d,
         tc.psum_pool(name="psum_z", bufs=3) as psum_z,
+        tc.psum_pool(name="psum_m", bufs=2) as psum_m,
     ):
         scratch = held.tile([P, 1], F32, name="scratch")
         nc.vector.memset(scratch[:], 0.0)
@@ -56,31 +57,34 @@ def tile_pgnn_layer_kernel(tc, x, dist, w1, b1, w2, wh, bh, offs, out):
             nc.sync.dma_start(b1_col[:], b1)
             load_dist(0)
             nc.sync.dma_start(w2_col[:], w2)
+            nc.sync.dma_start(bh_col[:], bh)
         nc.sync.dma_start(offsets[:], offs)
         for b in range(BLOCKS):
             nc.sync.dma_start(x_f32[b][:], x[b * P : (b + 1) * P, :])
         load_dist(1)
         nc.sync.dma_start(wh_sb[:], wh.rearrange("(k p) m -> p k m", p=P))
-        with nc.allow_non_contiguous_dma(reason="one element to a partition"):
-            nc.sync.dma_start(bh_col[:], bh)
         for k in range(2, PIECES):
             load_dist(k)
 
+        identity = held.tile([P, P], F32, name="identity")
+        make_identity(nc, identity[:])
         w2_wide = held.tile([P, M], BF16, name="w2_wide")
         nc.vector.tensor_copy(w2_wide[:], w2_col[:, 0:1].to_broadcast([P, M]))
         bh_quarter = held.tile([P, 1], F32, name="bh_quarter")
-        nc.gpsimd.tensor_scalar_mul(bh_quarter[:], bh_col[:], 0.25)
+        nc.vector.tensor_scalar_mul(bh_quarter[:], bh_col[:], 0.25)
 
         x_bf = [held.tile([P, S], BF16, name=f"x_bf_{b}") for b in range(BLOCKS)]
 
         def cast(b, dst, src):
             if b == 0:
-                nc.gpsimd.tensor_copy(dst, src)
+                nc.vector.tensor_copy(dst, src)
             else:
                 nc.scalar.activation(dst, src, COPY)
 
         d_ps = {}
         d_sb = {}
+        z_ps = {}
+        mean_ps = {}
 
         def start_d(k):
             hid = work.tile([P, PIECE], BF16, name="hid")
@@ -94,21 +98,9 @@ def tile_pgnn_layer_kernel(tc, x, dist, w1, b1, w2, wh, bh, offs, out):
             d_sb[k] = ahead.tile([P, PIECE], F32, name="d_sb")
             nc.scalar.activation(d_sb[k][:], d_ps[k][:], COPY, bias=0.25)
 
-        start_d(0)
-        for k in range(AHEAD):
-            start_d(k + 1)
-            finish_d(k)
-        for b in range(BLOCKS):
-            cast(b, x_bf[b][:], x_f32[b][:])
-
-        for k in range(PIECES):
-            if k + AHEAD + 1 < PIECES:
-                start_d(k + AHEAD + 1)
-            if k + AHEAD < PIECES:
-                finish_d(k + AHEAD)
-
-            z_ps = psum_z.tile([P, PIECE], F32, name="z_ps")
-            z_by_node = z_ps[:].rearrange("p (n a) -> p n a", a=A)
+        def gather_and_project(k):
+            z_ps[k] = psum_z.tile([P, PIECE], F32, name="z_ps")
+            z_by_node = z_ps[k][:].rearrange("p (n a) -> p n a", a=A)
             for b in range(BLOCKS):
                 own = x_bf[b][:, k * NODES : (k + 1) * NODES]
                 nc.tensor.matmul(
@@ -118,25 +110,49 @@ def tile_pgnn_layer_kernel(tc, x, dist, w1, b1, w2, wh, bh, offs, out):
                     start=(b == 0),
                     stop=False,
                 )
+            piece_offsets = offsets[:, k * (PIECE // 16) : (k + 1) * (PIECE // 16)]
+            msg = [work.tile([P, PIECE], F32, name=f"msg{b}") for b in range(BLOCKS)]
+            msg_bf = [work.tile([P, PIECE], BF16, name=f"msg_bf{b}") for b in range(BLOCKS)]
             for b in range(BLOCKS):
-                msg = work.tile([P, PIECE], F32, name=f"msg{b}")
                 nc.vector.tensor_tensor(
-                    msg[:],
-                    x_f32[b][:].indirect(offsets[:, k * (PIECE // 16) : (k + 1) * (PIECE // 16)]),
-                    d_sb[k][:],
-                    MULT,
+                    msg[b][:], x_f32[b][:].indirect(piece_offsets), d_sb[k][:], MULT
                 )
-                msg_bf = work.tile([P, PIECE], BF16, name=f"msg_bf{b}")
-                cast(b, msg_bf[:], msg[:])
+            for b in range(BLOCKS):
+                cast(b, msg_bf[b][:], msg[b][:])
                 nc.tensor.matmul(
-                    z_ps[:], wh_sb[:, b, :], msg_bf[:], start=False, stop=(b == BLOCKS - 1)
+                    z_ps[k][:], wh_sb[:, b, :], msg_bf[b][:], start=False, stop=(b == BLOCKS - 1)
                 )
 
+        def relu_and_mean(k):
             h = work.tile([P, PIECE], F32, name="h")
-            nc.scalar.activation(h[:], z_ps[:], RELU, bias=bh_quarter[:, 0:1], scale=0.25)
+            nc.scalar.activation(h[:], z_ps[k][:], RELU, bias=bh_quarter[:, 0:1], scale=0.25)
             h_by_node = h[:].rearrange("p (n a) -> p n a", a=A)
-            pair = work.tile([P, NODES, 2], F32, name="pair")
-            nc.gpsimd.tensor_tensor(pair[:], h_by_node[:, :, 0:2], h_by_node[:, :, 2:4], ADD)
+            mean_ps[k] = psum_m.tile([P, NODES], F32, name="mean_ps")
+            for a in range(A):
+                nc.tensor.matmul(
+                    mean_ps[k][:], identity[:], h_by_node[:, :, a], start=(a == 0), stop=(a == A - 1)
+                )
+
+        def store(k):
             mean = work.tile([P, NODES], F32, name="mean")
-            nc.gpsimd.tensor_tensor(mean[:], pair[:, :, 0], pair[:, :, 1], ADD)
+            nc.scalar.activation(mean[:], mean_ps[k][:], COPY)
             nc.sync.dma_start(out[:, k * NODES : (k + 1) * NODES], mean[:])
+
+        start_d(0)
+        for k in range(AHEAD):
+            start_d(k + 1)
+            finish_d(k)
+        for b in range(BLOCKS):
+            cast(b, x_bf[b][:], x_f32[b][:])
+
+        for t in range(PIECES + 2):
+            if t + AHEAD + 1 < PIECES:
+                start_d(t + AHEAD + 1)
+            if t + AHEAD < PIECES:
+                finish_d(t + AHEAD)
+            if 0 <= t - 1 < PIECES:
+                relu_and_mean(t - 1)
+            if 0 <= t - 2:
+                store(t - 2)
+            if t < PIECES:
+                gather_and_project(t)

@@ -55,15 +55,16 @@ def tile_pgnn_layer_kernel(tc, x, dist, w1, b1, w2, wh, bh, offs, out):
         with nc.allow_non_contiguous_dma(reason="one element to a partition"):
             nc.sync.dma_start(w1_col[:], w1)
             nc.sync.dma_start(b1_col[:], b1)
-            load_dist(0)
             nc.sync.dma_start(w2_col[:], w2)
+            load_dist(0)
+            load_dist(1)
             nc.sync.dma_start(bh_col[:], bh)
         nc.sync.dma_start(offsets[:], offs)
-        for b in range(BLOCKS):
-            nc.sync.dma_start(x_f32[b][:], x[b * P : (b + 1) * P, :])
-        load_dist(1)
+        nc.sync.dma_start(x_f32[0][:], x[0:P, :])
+        load_dist(2)
+        nc.sync.dma_start(x_f32[1][:], x[P : 2 * P, :])
         nc.sync.dma_start(wh_sb[:], wh.rearrange("(k p) m -> p k m", p=P))
-        for k in range(2, PIECES):
+        for k in range(3, PIECES):
             load_dist(k)
 
         identity = held.tile([P, P], F32, name="identity")
@@ -84,6 +85,7 @@ def tile_pgnn_layer_kernel(tc, x, dist, w1, b1, w2, wh, bh, offs, out):
         d_ps = {}
         d_sb = {}
         z_ps = {}
+        h = {}
         mean_ps = {}
 
         def start_d(k):
@@ -99,6 +101,15 @@ def tile_pgnn_layer_kernel(tc, x, dist, w1, b1, w2, wh, bh, offs, out):
             nc.scalar.activation(d_sb[k][:], d_ps[k][:], COPY, bias=0.25)
 
         def gather_and_project(k):
+            piece_offsets = offsets[:, k * (PIECE // 16) : (k + 1) * (PIECE // 16)]
+            msg = [work.tile([P, PIECE], F32, name=f"msg{b}") for b in range(BLOCKS)]
+            msg_bf = [work.tile([P, PIECE], BF16, name=f"msg_bf{b}") for b in range(BLOCKS)]
+            for b in range(BLOCKS):
+                nc.vector.tensor_tensor(
+                    msg[b][:], x_f32[b][:].indirect(piece_offsets), d_sb[k][:], MULT
+                )
+            for b in range(BLOCKS):
+                cast(b, msg_bf[b][:], msg[b][:])
             z_ps[k] = psum_z.tile([P, PIECE], F32, name="z_ps")
             z_by_node = z_ps[k][:].rearrange("p (n a) -> p n a", a=A)
             for b in range(BLOCKS):
@@ -110,23 +121,17 @@ def tile_pgnn_layer_kernel(tc, x, dist, w1, b1, w2, wh, bh, offs, out):
                     start=(b == 0),
                     stop=False,
                 )
-            piece_offsets = offsets[:, k * (PIECE // 16) : (k + 1) * (PIECE // 16)]
-            msg = [work.tile([P, PIECE], F32, name=f"msg{b}") for b in range(BLOCKS)]
-            msg_bf = [work.tile([P, PIECE], BF16, name=f"msg_bf{b}") for b in range(BLOCKS)]
             for b in range(BLOCKS):
-                nc.vector.tensor_tensor(
-                    msg[b][:], x_f32[b][:].indirect(piece_offsets), d_sb[k][:], MULT
-                )
-            for b in range(BLOCKS):
-                cast(b, msg_bf[b][:], msg[b][:])
                 nc.tensor.matmul(
                     z_ps[k][:], wh_sb[:, b, :], msg_bf[b][:], start=False, stop=(b == BLOCKS - 1)
                 )
 
-        def relu_and_mean(k):
-            h = work.tile([P, PIECE], F32, name="h")
-            nc.scalar.activation(h[:], z_ps[k][:], RELU, bias=bh_quarter[:, 0:1], scale=0.25)
-            h_by_node = h[:].rearrange("p (n a) -> p n a", a=A)
+        def relu(k):
+            h[k] = work.tile([P, PIECE], F32, name="h")
+            nc.scalar.activation(h[k][:], z_ps[k][:], RELU, bias=bh_quarter[:, 0:1], scale=0.25)
+
+        def add_anchors(k):
+            h_by_node = h[k][:].rearrange("p (n a) -> p n a", a=A)
             mean_ps[k] = psum_m.tile([P, NODES], F32, name="mean_ps")
             for a in range(A):
                 nc.tensor.matmul(
@@ -139,11 +144,12 @@ def tile_pgnn_layer_kernel(tc, x, dist, w1, b1, w2, wh, bh, offs, out):
             nc.sync.dma_start(out[:, k * NODES : (k + 1) * NODES], mean[:])
 
         start_d(0)
-        for k in range(AHEAD):
-            start_d(k + 1)
-            finish_d(k)
-        for b in range(BLOCKS):
-            cast(b, x_bf[b][:], x_f32[b][:])
+        start_d(1)
+        finish_d(0)
+        cast(0, x_bf[0][:], x_f32[0][:])
+        start_d(2)
+        finish_d(1)
+        cast(1, x_bf[1][:], x_f32[1][:])
 
         for t in range(PIECES + 2):
             if t + AHEAD + 1 < PIECES:
@@ -151,8 +157,10 @@ def tile_pgnn_layer_kernel(tc, x, dist, w1, b1, w2, wh, bh, offs, out):
             if t + AHEAD < PIECES:
                 finish_d(t + AHEAD)
             if 0 <= t - 1 < PIECES:
-                relu_and_mean(t - 1)
+                relu(t - 1)
             if 0 <= t - 2:
                 store(t - 2)
             if t < PIECES:
                 gather_and_project(t)
+            if 0 <= t - 1 < PIECES:
+                add_anchors(t - 1)

@@ -1,5 +1,4 @@
 import concourse.mybir as mybir
-from concourse.masks import make_identity
 
 F32 = mybir.dt.float32
 BF16 = mybir.dt.bfloat16
@@ -7,6 +6,8 @@ U16 = mybir.dt.uint16
 RELU = mybir.ActivationFunctionType.Relu
 COPY = mybir.ActivationFunctionType.Copy
 MULT = mybir.AluOpType.mult
+ADD = mybir.AluOpType.add
+X_AXIS = mybir.AxisListType.X
 
 P = 128
 C = 256
@@ -18,7 +19,6 @@ BLOCKS = C // P
 PIECE = 512
 PIECES = N // PIECE
 NODES = PIECE // A
-AHEAD = 2
 
 FLOPS = 2 * M * C * N + 2 * M * C * S + 2 * M * N
 
@@ -28,10 +28,10 @@ def tile_pgnn_layer_kernel(tc, x, dist, w1, b1, w2, wh, bh, offs, out):
     with (
         tc.tile_pool(name="held", bufs=1) as held,
         tc.tile_pool(name="work", bufs=3) as work,
-        tc.tile_pool(name="ahead", bufs=AHEAD + 2) as ahead,
+        tc.tile_pool(name="ahead", bufs=4) as ahead,
+        tc.psum_pool(name="psum_dist", bufs=2) as psum_dist,
         tc.psum_pool(name="psum_d", bufs=2) as psum_d,
         tc.psum_pool(name="psum_z", bufs=3) as psum_z,
-        tc.psum_pool(name="psum_m", bufs=2) as psum_m,
     ):
         scratch = held.tile([P, 1], F32, name="scratch")
         nc.vector.memset(scratch[:], 0.0)
@@ -41,34 +41,24 @@ def tile_pgnn_layer_kernel(tc, x, dist, w1, b1, w2, wh, bh, offs, out):
         b1_col = held.tile([P, 1], F32, name="b1_col")
         w2_col = held.tile([P, 1], BF16, name="w2_col")
         bh_col = held.tile([P, 1], F32, name="bh_col")
+        dist_row = held.tile([1, N], F32, name="dist_row")
         wh_sb = held.tile([P, 2 * BLOCKS, M], BF16, name="wh_sb")
         offsets = held.tile([P, N // 16], U16, name="offsets")
         x_f32 = [held.tile([P, S], F32, name=f"x_f32_{b}") for b in range(BLOCKS)]
-        dist_row = dist.rearrange("o n -> (o n)")
-        dist_all = [held.tile([P, PIECE], F32, name=f"dist_all{k}") for k in range(PIECES)]
 
-        def load_dist(k):
-            nc.sync.dma_start(
-                dist_all[k][:], dist_row[k * PIECE : (k + 1) * PIECE].partition_broadcast(P)
-            )
-
+        nc.sync.dma_start(dist_row[:], dist)
         with nc.allow_non_contiguous_dma(reason="one element to a partition"):
             nc.sync.dma_start(w1_col[:], w1)
             nc.sync.dma_start(b1_col[:], b1)
             nc.sync.dma_start(w2_col[:], w2)
-            load_dist(0)
-            load_dist(1)
             nc.sync.dma_start(bh_col[:], bh)
         nc.sync.dma_start(offsets[:], offs)
-        nc.sync.dma_start(x_f32[0][:], x[0:P, :])
-        load_dist(2)
-        nc.sync.dma_start(x_f32[1][:], x[P : 2 * P, :])
+        for b in range(BLOCKS):
+            nc.sync.dma_start(x_f32[b][:], x[b * P : (b + 1) * P, :])
         nc.sync.dma_start(wh_sb[:], wh.rearrange("(k p) m -> p k m", p=P))
-        for k in range(3, PIECES):
-            load_dist(k)
 
-        identity = held.tile([P, P], F32, name="identity")
-        make_identity(nc, identity[:])
+        ones_row = held.tile([1, P], F32, name="ones_row")
+        nc.vector.memset(ones_row[:], 1.0)
         w2_wide = held.tile([P, M], BF16, name="w2_wide")
         nc.vector.tensor_copy(w2_wide[:], w2_col[:, 0:1].to_broadcast([P, M]))
         bh_quarter = held.tile([P, 1], F32, name="bh_quarter")
@@ -76,22 +66,23 @@ def tile_pgnn_layer_kernel(tc, x, dist, w1, b1, w2, wh, bh, offs, out):
 
         x_bf = [held.tile([P, S], BF16, name=f"x_bf_{b}") for b in range(BLOCKS)]
 
-        def cast(b, dst, src):
-            if b == 0:
-                nc.vector.tensor_copy(dst, src)
-            else:
-                nc.scalar.activation(dst, src, COPY)
-
+        dist_ps = {}
         d_ps = {}
         d_sb = {}
         z_ps = {}
         h = {}
-        mean_ps = {}
+
+        def spread_dist(k):
+            dist_ps[k] = psum_dist.tile([P, PIECE], F32, name="dist_ps")
+            nc.tensor.matmul(
+                dist_ps[k][:], ones_row[:], dist_row[:, k * PIECE : (k + 1) * PIECE],
+                start=True, stop=True,
+            )
 
         def start_d(k):
             hid = work.tile([P, PIECE], BF16, name="hid")
             nc.scalar.activation(
-                hid[:], dist_all[k][:], RELU, bias=b1_col[:, 0:1], scale=w1_col[:, 0:1]
+                hid[:], dist_ps[k][:], RELU, bias=b1_col[:, 0:1], scale=w1_col[:, 0:1]
             )
             d_ps[k] = psum_d.tile([P, PIECE], F32, name="d_ps")
             nc.tensor.matmul(d_ps[k][:], w2_wide[:], hid[:], start=True, stop=True)
@@ -100,16 +91,20 @@ def tile_pgnn_layer_kernel(tc, x, dist, w1, b1, w2, wh, bh, offs, out):
             d_sb[k] = ahead.tile([P, PIECE], F32, name="d_sb")
             nc.scalar.activation(d_sb[k][:], d_ps[k][:], COPY, bias=0.25)
 
-        def gather_and_project(k):
+        msg = {}
+
+        def gather(k):
             piece_offsets = offsets[:, k * (PIECE // 16) : (k + 1) * (PIECE // 16)]
-            msg = [work.tile([P, PIECE], F32, name=f"msg{b}") for b in range(BLOCKS)]
-            msg_bf = [work.tile([P, PIECE], BF16, name=f"msg_bf{b}") for b in range(BLOCKS)]
+            msg[k] = [work.tile([P, PIECE], F32, name=f"msg{b}") for b in range(BLOCKS)]
             for b in range(BLOCKS):
                 nc.vector.tensor_tensor(
-                    msg[b][:], x_f32[b][:].indirect(piece_offsets), d_sb[k][:], MULT
+                    msg[k][b][:], x_f32[b][:].indirect(piece_offsets), d_sb[k][:], MULT
                 )
+
+        def project(k):
+            msg_bf = [work.tile([P, PIECE], BF16, name=f"msg_bf{b}") for b in range(BLOCKS)]
             for b in range(BLOCKS):
-                cast(b, msg_bf[b][:], msg[b][:])
+                nc.scalar.activation(msg_bf[b][:], msg[k][b][:], COPY)
             z_ps[k] = psum_z.tile([P, PIECE], F32, name="z_ps")
             z_by_node = z_ps[k][:].rearrange("p (n a) -> p n a", a=A)
             for b in range(BLOCKS):
@@ -130,37 +125,37 @@ def tile_pgnn_layer_kernel(tc, x, dist, w1, b1, w2, wh, bh, offs, out):
             h[k] = work.tile([P, PIECE], F32, name="h")
             nc.scalar.activation(h[k][:], z_ps[k][:], RELU, bias=bh_quarter[:, 0:1], scale=0.25)
 
-        def add_anchors(k):
-            h_by_node = h[k][:].rearrange("p (n a) -> p n a", a=A)
-            mean_ps[k] = psum_m.tile([P, NODES], F32, name="mean_ps")
-            for a in range(A):
-                nc.tensor.matmul(
-                    mean_ps[k][:], identity[:], h_by_node[:, :, a], start=(a == 0), stop=(a == A - 1)
-                )
-
-        def store(k):
+        def mean_and_store(k):
             mean = work.tile([P, NODES], F32, name="mean")
-            nc.scalar.activation(mean[:], mean_ps[k][:], COPY)
+            nc.vector.tensor_reduce(
+                mean[:], h[k][:].rearrange("p (n a) -> p n a", a=A), axis=X_AXIS, op=ADD
+            )
             nc.sync.dma_start(out[:, k * NODES : (k + 1) * NODES], mean[:])
 
+        spread_dist(0)
+        spread_dist(1)
         start_d(0)
+        spread_dist(2)
         start_d(1)
         finish_d(0)
-        cast(0, x_bf[0][:], x_f32[0][:])
+        spread_dist(3)
         start_d(2)
         finish_d(1)
-        cast(1, x_bf[1][:], x_f32[1][:])
+        for b in range(BLOCKS):
+            nc.vector.tensor_copy(x_bf[b][:], x_f32[b][:])
 
         for t in range(PIECES + 2):
-            if t + AHEAD + 1 < PIECES:
-                start_d(t + AHEAD + 1)
-            if t + AHEAD < PIECES:
-                finish_d(t + AHEAD)
+            if t + 4 < PIECES:
+                spread_dist(t + 4)
+            if t + 3 < PIECES:
+                start_d(t + 3)
+            if t + 2 < PIECES:
+                finish_d(t + 2)
             if 0 <= t - 1 < PIECES:
                 relu(t - 1)
-            if 0 <= t - 2:
-                store(t - 2)
             if t < PIECES:
-                gather_and_project(t)
-            if 0 <= t - 1 < PIECES:
-                add_anchors(t - 1)
+                gather(t)
+            if 0 <= t - 2:
+                mean_and_store(t - 2)
+            if t < PIECES:
+                project(t)

@@ -1,4 +1,5 @@
 import concourse.mybir as mybir
+from concourse.masks import make_identity
 
 F32 = mybir.dt.float32
 BF16 = mybir.dt.bfloat16
@@ -6,8 +7,6 @@ U16 = mybir.dt.uint16
 RELU = mybir.ActivationFunctionType.Relu
 COPY = mybir.ActivationFunctionType.Copy
 MULT = mybir.AluOpType.mult
-ADD = mybir.AluOpType.add
-X_AXIS = mybir.AxisListType.X
 
 P = 128
 C = 256
@@ -19,6 +18,7 @@ BLOCKS = C // P
 PIECE = 512
 PIECES = N // PIECE
 NODES = PIECE // A
+AHEAD = 2
 
 FLOPS = 2 * M * C * N + 2 * M * C * S + 2 * M * N
 
@@ -28,10 +28,10 @@ def tile_pgnn_layer_kernel(tc, x, dist, w1, b1, w2, wh, bh, offs, out):
     with (
         tc.tile_pool(name="held", bufs=1) as held,
         tc.tile_pool(name="work", bufs=3) as work,
-        tc.tile_pool(name="ahead", bufs=4) as ahead,
-        tc.psum_pool(name="psum_dist", bufs=2) as psum_dist,
+        tc.tile_pool(name="ahead", bufs=AHEAD + 2) as ahead,
         tc.psum_pool(name="psum_d", bufs=2) as psum_d,
         tc.psum_pool(name="psum_z", bufs=3) as psum_z,
+        tc.psum_pool(name="psum_m", bufs=2) as psum_m,
     ):
         scratch = held.tile([P, 1], F32, name="scratch")
         nc.vector.memset(scratch[:], 0.0)
@@ -41,24 +41,35 @@ def tile_pgnn_layer_kernel(tc, x, dist, w1, b1, w2, wh, bh, offs, out):
         b1_col = held.tile([P, 1], F32, name="b1_col")
         w2_col = held.tile([P, 1], BF16, name="w2_col")
         bh_col = held.tile([P, 1], F32, name="bh_col")
-        dist_row = held.tile([1, N], F32, name="dist_row")
         wh_sb = held.tile([P, 2 * BLOCKS, M], BF16, name="wh_sb")
         offsets = held.tile([P, N // 16], U16, name="offsets")
         x_f32 = [held.tile([P, S], F32, name=f"x_f32_{b}") for b in range(BLOCKS)]
+        dist_row = dist.rearrange("o n -> (o n)")
+        dist_all = [held.tile([P, PIECE], F32, name=f"dist_all{k}") for k in range(PIECES)]
 
-        nc.sync.dma_start(dist_row[:], dist)
+        def load_dist(k):
+            queue = nc.sync if k % 2 == 0 else nc.scalar
+            queue.dma_start(
+                dist_all[k][:], dist_row[k * PIECE : (k + 1) * PIECE].partition_broadcast(P)
+            )
+
         with nc.allow_non_contiguous_dma(reason="one element to a partition"):
             nc.sync.dma_start(w1_col[:], w1)
             nc.sync.dma_start(b1_col[:], b1)
             nc.sync.dma_start(w2_col[:], w2)
+            load_dist(0)
+            load_dist(1)
             nc.sync.dma_start(bh_col[:], bh)
         nc.sync.dma_start(offsets[:], offs)
-        for b in range(BLOCKS):
-            nc.sync.dma_start(x_f32[b][:], x[b * P : (b + 1) * P, :])
+        nc.sync.dma_start(x_f32[0][:], x[0:P, :])
+        load_dist(2)
+        nc.sync.dma_start(x_f32[1][:], x[P : 2 * P, :])
         nc.sync.dma_start(wh_sb[:], wh.rearrange("(k p) m -> p k m", p=P))
+        for k in range(3, PIECES):
+            load_dist(k)
 
-        ones_row = held.tile([1, P], F32, name="ones_row")
-        nc.vector.memset(ones_row[:], 1.0)
+        identity = held.tile([P, P], F32, name="identity")
+        make_identity(nc, identity[:])
         w2_wide = held.tile([P, M], BF16, name="w2_wide")
         nc.vector.tensor_copy(w2_wide[:], w2_col[:, 0:1].to_broadcast([P, M]))
         bh_quarter = held.tile([P, 1], F32, name="bh_quarter")
@@ -66,23 +77,22 @@ def tile_pgnn_layer_kernel(tc, x, dist, w1, b1, w2, wh, bh, offs, out):
 
         x_bf = [held.tile([P, S], BF16, name=f"x_bf_{b}") for b in range(BLOCKS)]
 
-        dist_ps = {}
+        def cast(b, dst, src):
+            if b == 0:
+                nc.vector.tensor_copy(dst, src)
+            else:
+                nc.scalar.activation(dst, src, COPY)
+
         d_ps = {}
         d_sb = {}
         z_ps = {}
         h = {}
-
-        def spread_dist(k):
-            dist_ps[k] = psum_dist.tile([P, PIECE], F32, name="dist_ps")
-            nc.tensor.matmul(
-                dist_ps[k][:], ones_row[:], dist_row[:, k * PIECE : (k + 1) * PIECE],
-                start=True, stop=True,
-            )
+        mean_ps = {}
 
         def start_d(k):
             hid = work.tile([P, PIECE], BF16, name="hid")
             nc.scalar.activation(
-                hid[:], dist_ps[k][:], RELU, bias=b1_col[:, 0:1], scale=w1_col[:, 0:1]
+                hid[:], dist_all[k][:], RELU, bias=b1_col[:, 0:1], scale=w1_col[:, 0:1]
             )
             d_ps[k] = psum_d.tile([P, PIECE], F32, name="d_ps")
             nc.tensor.matmul(d_ps[k][:], w2_wide[:], hid[:], start=True, stop=True)
@@ -91,20 +101,16 @@ def tile_pgnn_layer_kernel(tc, x, dist, w1, b1, w2, wh, bh, offs, out):
             d_sb[k] = ahead.tile([P, PIECE], F32, name="d_sb")
             nc.scalar.activation(d_sb[k][:], d_ps[k][:], COPY, bias=0.25)
 
-        msg = {}
-
-        def gather(k):
+        def gather_and_project(k):
             piece_offsets = offsets[:, k * (PIECE // 16) : (k + 1) * (PIECE // 16)]
-            msg[k] = [work.tile([P, PIECE], F32, name=f"msg{b}") for b in range(BLOCKS)]
-            for b in range(BLOCKS):
-                nc.vector.tensor_tensor(
-                    msg[k][b][:], x_f32[b][:].indirect(piece_offsets), d_sb[k][:], MULT
-                )
-
-        def project(k):
+            msg = [work.tile([P, PIECE], F32, name=f"msg{b}") for b in range(BLOCKS)]
             msg_bf = [work.tile([P, PIECE], BF16, name=f"msg_bf{b}") for b in range(BLOCKS)]
             for b in range(BLOCKS):
-                nc.scalar.activation(msg_bf[b][:], msg[k][b][:], COPY)
+                nc.vector.tensor_tensor(
+                    msg[b][:], x_f32[b][:].indirect(piece_offsets), d_sb[k][:], MULT
+                )
+            for b in range(BLOCKS):
+                cast(b, msg_bf[b][:], msg[b][:])
             z_ps[k] = psum_z.tile([P, PIECE], F32, name="z_ps")
             z_by_node = z_ps[k][:].rearrange("p (n a) -> p n a", a=A)
             for b in range(BLOCKS):
@@ -125,37 +131,37 @@ def tile_pgnn_layer_kernel(tc, x, dist, w1, b1, w2, wh, bh, offs, out):
             h[k] = work.tile([P, PIECE], F32, name="h")
             nc.scalar.activation(h[k][:], z_ps[k][:], RELU, bias=bh_quarter[:, 0:1], scale=0.25)
 
-        def mean_and_store(k):
+        def add_anchors(k):
+            h_by_node = h[k][:].rearrange("p (n a) -> p n a", a=A)
+            mean_ps[k] = psum_m.tile([P, NODES], F32, name="mean_ps")
+            for a in range(A):
+                nc.tensor.matmul(
+                    mean_ps[k][:], identity[:], h_by_node[:, :, a], start=(a == 0), stop=(a == A - 1)
+                )
+
+        def store(k):
             mean = work.tile([P, NODES], F32, name="mean")
-            nc.vector.tensor_reduce(
-                mean[:], h[k][:].rearrange("p (n a) -> p n a", a=A), axis=X_AXIS, op=ADD
-            )
+            nc.scalar.activation(mean[:], mean_ps[k][:], COPY)
             nc.sync.dma_start(out[:, k * NODES : (k + 1) * NODES], mean[:])
 
-        spread_dist(0)
-        spread_dist(1)
         start_d(0)
-        spread_dist(2)
         start_d(1)
         finish_d(0)
-        spread_dist(3)
+        cast(0, x_bf[0][:], x_f32[0][:])
         start_d(2)
         finish_d(1)
-        for b in range(BLOCKS):
-            nc.vector.tensor_copy(x_bf[b][:], x_f32[b][:])
+        cast(1, x_bf[1][:], x_f32[1][:])
 
         for t in range(PIECES + 2):
-            if t + 4 < PIECES:
-                spread_dist(t + 4)
-            if t + 3 < PIECES:
-                start_d(t + 3)
-            if t + 2 < PIECES:
-                finish_d(t + 2)
+            if t + AHEAD + 1 < PIECES:
+                start_d(t + AHEAD + 1)
+            if t + AHEAD < PIECES:
+                finish_d(t + AHEAD)
             if 0 <= t - 1 < PIECES:
                 relu(t - 1)
-            if t < PIECES:
-                gather(t)
             if 0 <= t - 2:
-                mean_and_store(t - 2)
+                store(t - 2)
             if t < PIECES:
-                project(t)
+                gather_and_project(t)
+            if 0 <= t - 1 < PIECES:
+                add_anchors(t - 1)

@@ -1,5 +1,4 @@
 import concourse.mybir as mybir
-from concourse.masks import make_identity
 
 F32 = mybir.dt.float32
 BF16 = mybir.dt.bfloat16
@@ -7,6 +6,7 @@ U16 = mybir.dt.uint16
 RELU = mybir.ActivationFunctionType.Relu
 COPY = mybir.ActivationFunctionType.Copy
 MULT = mybir.AluOpType.mult
+ADD = mybir.AluOpType.add
 
 P = 128
 C = 256
@@ -18,7 +18,6 @@ BLOCKS = C // P
 PIECE = 512
 PIECES = N // PIECE
 NODES = PIECE // A
-AHEAD = 2
 
 FLOPS = 2 * M * C * N + 2 * M * C * S + 2 * M * N
 
@@ -28,48 +27,48 @@ def tile_pgnn_layer_kernel(tc, x, dist, w1, b1, w2, wh, bh, offs, out):
     with (
         tc.tile_pool(name="held", bufs=1) as held,
         tc.tile_pool(name="work", bufs=3) as work,
-        tc.tile_pool(name="ahead", bufs=AHEAD + 2) as ahead,
+        tc.tile_pool(name="ahead", bufs=4) as ahead,
+        tc.psum_pool(name="psum_dist", bufs=2) as psum_dist,
         tc.psum_pool(name="psum_d", bufs=2) as psum_d,
         tc.psum_pool(name="psum_z", bufs=3) as psum_z,
-        tc.psum_pool(name="psum_m", bufs=2) as psum_m,
     ):
-        scratch = held.tile([P, 1], F32, name="scratch")
-        nc.vector.memset(scratch[:], 0.0)
-        nc.scalar.activation(scratch[:], scratch[:], RELU)
-
         w1_col = held.tile([P, 1], F32, name="w1_col")
         b1_col = held.tile([P, 1], F32, name="b1_col")
         w2_col = held.tile([P, 1], BF16, name="w2_col")
         bh_col = held.tile([P, 1], F32, name="bh_col")
+        dist_pad = held.tile([P, N], F32, name="dist_pad")
         wh_sb = held.tile([P, 2 * BLOCKS, M], BF16, name="wh_sb")
         offsets = held.tile([P, N // 16], U16, name="offsets")
         x_f32 = [held.tile([P, S], F32, name=f"x_f32_{b}") for b in range(BLOCKS)]
-        dist_row = dist.rearrange("o n -> (o n)")
-        dist_all = [held.tile([P, PIECE], F32, name=f"dist_all{k}") for k in range(PIECES)]
+
+        def piece(k):
+            return slice(k * PIECE, (k + 1) * PIECE)
 
         def load_dist(k):
-            queue = nc.sync if k % 2 == 0 else nc.scalar
-            queue.dma_start(
-                dist_all[k][:], dist_row[k * PIECE : (k + 1) * PIECE].partition_broadcast(P)
-            )
+            nc.vector.memset(dist_pad[:, piece(k)], 0.0)
+            nc.scalar.dma_start(dist_pad[0:1, piece(k)], dist[:, piece(k)])
+
+        load_dist(0)
+        load_dist(1)
+        scratch = held.tile([P, 1], F32, name="scratch")
+        nc.gpsimd.memset(scratch[:], 0.0)
+        nc.scalar.activation(scratch[:], scratch[:], RELU)
+        for k in range(2, PIECES):
+            load_dist(k)
 
         with nc.allow_non_contiguous_dma(reason="one element to a partition"):
             nc.sync.dma_start(w1_col[:], w1)
             nc.sync.dma_start(b1_col[:], b1)
             nc.sync.dma_start(w2_col[:], w2)
-            load_dist(0)
-            load_dist(1)
             nc.sync.dma_start(bh_col[:], bh)
         nc.sync.dma_start(offsets[:], offs)
-        nc.sync.dma_start(x_f32[0][:], x[0:P, :])
-        load_dist(2)
-        nc.sync.dma_start(x_f32[1][:], x[P : 2 * P, :])
+        for b in range(BLOCKS):
+            nc.sync.dma_start(x_f32[b][:], x[b * P : (b + 1) * P, :])
         nc.sync.dma_start(wh_sb[:], wh.rearrange("(k p) m -> p k m", p=P))
-        for k in range(3, PIECES):
-            load_dist(k)
 
-        identity = held.tile([P, P], F32, name="identity")
-        make_identity(nc, identity[:])
+        pick_row0 = held.tile([P, P], F32, name="pick_row0")
+        nc.gpsimd.memset(pick_row0[:], 0.0)
+        nc.gpsimd.memset(pick_row0[0:1, :], 1.0)
         w2_wide = held.tile([P, M], BF16, name="w2_wide")
         nc.vector.tensor_copy(w2_wide[:], w2_col[:, 0:1].to_broadcast([P, M]))
         bh_quarter = held.tile([P, 1], F32, name="bh_quarter")
@@ -77,22 +76,20 @@ def tile_pgnn_layer_kernel(tc, x, dist, w1, b1, w2, wh, bh, offs, out):
 
         x_bf = [held.tile([P, S], BF16, name=f"x_bf_{b}") for b in range(BLOCKS)]
 
-        def cast(b, dst, src):
-            if b == 0:
-                nc.vector.tensor_copy(dst, src)
-            else:
-                nc.scalar.activation(dst, src, COPY)
-
+        dist_ps = {}
         d_ps = {}
         d_sb = {}
         z_ps = {}
         h = {}
-        mean_ps = {}
+
+        def spread_dist(k):
+            dist_ps[k] = psum_dist.tile([P, PIECE], F32, name="dist_ps")
+            nc.tensor.matmul(dist_ps[k][:], pick_row0[:], dist_pad[:, piece(k)], start=True, stop=True)
 
         def start_d(k):
             hid = work.tile([P, PIECE], BF16, name="hid")
             nc.scalar.activation(
-                hid[:], dist_all[k][:], RELU, bias=b1_col[:, 0:1], scale=w1_col[:, 0:1]
+                hid[:], dist_ps[k][:], RELU, bias=b1_col[:, 0:1], scale=w1_col[:, 0:1]
             )
             d_ps[k] = psum_d.tile([P, PIECE], F32, name="d_ps")
             nc.tensor.matmul(d_ps[k][:], w2_wide[:], hid[:], start=True, stop=True)
@@ -101,16 +98,20 @@ def tile_pgnn_layer_kernel(tc, x, dist, w1, b1, w2, wh, bh, offs, out):
             d_sb[k] = ahead.tile([P, PIECE], F32, name="d_sb")
             nc.scalar.activation(d_sb[k][:], d_ps[k][:], COPY, bias=0.25)
 
-        def gather_and_project(k):
+        msg = {}
+
+        def gather(k):
             piece_offsets = offsets[:, k * (PIECE // 16) : (k + 1) * (PIECE // 16)]
-            msg = [work.tile([P, PIECE], F32, name=f"msg{b}") for b in range(BLOCKS)]
-            msg_bf = [work.tile([P, PIECE], BF16, name=f"msg_bf{b}") for b in range(BLOCKS)]
+            msg[k] = [work.tile([P, PIECE], F32, name=f"msg{b}") for b in range(BLOCKS)]
             for b in range(BLOCKS):
                 nc.vector.tensor_tensor(
-                    msg[b][:], x_f32[b][:].indirect(piece_offsets), d_sb[k][:], MULT
+                    msg[k][b][:], x_f32[b][:].indirect(piece_offsets), d_sb[k][:], MULT
                 )
+
+        def project(k):
+            msg_bf = [work.tile([P, PIECE], BF16, name=f"msg_bf{b}") for b in range(BLOCKS)]
             for b in range(BLOCKS):
-                cast(b, msg_bf[b][:], msg[b][:])
+                nc.scalar.activation(msg_bf[b][:], msg[k][b][:], COPY)
             z_ps[k] = psum_z.tile([P, PIECE], F32, name="z_ps")
             z_by_node = z_ps[k][:].rearrange("p (n a) -> p n a", a=A)
             for b in range(BLOCKS):
@@ -131,37 +132,37 @@ def tile_pgnn_layer_kernel(tc, x, dist, w1, b1, w2, wh, bh, offs, out):
             h[k] = work.tile([P, PIECE], F32, name="h")
             nc.scalar.activation(h[k][:], z_ps[k][:], RELU, bias=bh_quarter[:, 0:1], scale=0.25)
 
-        def add_anchors(k):
+        def mean_and_store(k):
             h_by_node = h[k][:].rearrange("p (n a) -> p n a", a=A)
-            mean_ps[k] = psum_m.tile([P, NODES], F32, name="mean_ps")
-            for a in range(A):
-                nc.tensor.matmul(
-                    mean_ps[k][:], identity[:], h_by_node[:, :, a], start=(a == 0), stop=(a == A - 1)
-                )
-
-        def store(k):
+            pair = work.tile([P, NODES, 2], F32, name="pair")
+            nc.gpsimd.tensor_tensor(pair[:], h_by_node[:, :, 0:2], h_by_node[:, :, 2:4], ADD)
             mean = work.tile([P, NODES], F32, name="mean")
-            nc.scalar.activation(mean[:], mean_ps[k][:], COPY)
+            nc.gpsimd.tensor_tensor(mean[:], pair[:, :, 0], pair[:, :, 1], ADD)
             nc.sync.dma_start(out[:, k * NODES : (k + 1) * NODES], mean[:])
 
+        spread_dist(0)
+        spread_dist(1)
         start_d(0)
+        spread_dist(2)
         start_d(1)
         finish_d(0)
-        cast(0, x_bf[0][:], x_f32[0][:])
+        spread_dist(3)
         start_d(2)
         finish_d(1)
-        cast(1, x_bf[1][:], x_f32[1][:])
+        for b in range(BLOCKS):
+            nc.vector.tensor_copy(x_bf[b][:], x_f32[b][:])
 
-        for t in range(PIECES + 2):
-            if t + AHEAD + 1 < PIECES:
-                start_d(t + AHEAD + 1)
-            if t + AHEAD < PIECES:
-                finish_d(t + AHEAD)
+        for t in range(PIECES + 1):
+            if t + 4 < PIECES:
+                spread_dist(t + 4)
+            if t + 3 < PIECES:
+                start_d(t + 3)
+            if t + 2 < PIECES:
+                finish_d(t + 2)
             if 0 <= t - 1 < PIECES:
                 relu(t - 1)
-            if 0 <= t - 2:
-                store(t - 2)
+                mean_and_store(t - 1)
             if t < PIECES:
-                gather_and_project(t)
-            if 0 <= t - 1 < PIECES:
-                add_anchors(t - 1)
+                gather(t)
+            if t < PIECES:
+                project(t)

@@ -7,6 +7,7 @@ RELU = mybir.ActivationFunctionType.Relu
 COPY = mybir.ActivationFunctionType.Copy
 MULT = mybir.AluOpType.mult
 ADD = mybir.AluOpType.add
+X_AXIS = mybir.AxisListType.X
 
 P = 128
 C = 256
@@ -133,11 +134,10 @@ def tile_pgnn_layer_kernel(tc, x, dist, w1, b1, w2, wh, bh, offs, out):
             nc.scalar.activation(h[k][:], z_ps[k][:], RELU, bias=bh_quarter[:, 0:1], scale=0.25)
 
         def mean_and_store(k):
-            h_by_node = h[k][:].rearrange("p (n a) -> p n a", a=A)
-            pair = work.tile([P, NODES, 2], F32, name="pair")
-            nc.gpsimd.tensor_tensor(pair[:], h_by_node[:, :, 0:2], h_by_node[:, :, 2:4], ADD)
             mean = work.tile([P, NODES], F32, name="mean")
-            nc.gpsimd.tensor_tensor(mean[:], pair[:, :, 0], pair[:, :, 1], ADD)
+            nc.vector.tensor_reduce(
+                mean[:], h[k][:].rearrange("p (n a) -> p n a", a=A), axis=X_AXIS, op=ADD
+            )
             nc.sync.dma_start(out[:, k * NODES : (k + 1) * NODES], mean[:])
 
         spread_dist(0)
@@ -152,7 +152,7 @@ def tile_pgnn_layer_kernel(tc, x, dist, w1, b1, w2, wh, bh, offs, out):
         for b in range(BLOCKS):
             nc.vector.tensor_copy(x_bf[b][:], x_f32[b][:])
 
-        for t in range(PIECES + 1):
+        for t in range(PIECES + 2):
             if t + 4 < PIECES:
                 spread_dist(t + 4)
             if t + 3 < PIECES:
@@ -161,8 +161,9 @@ def tile_pgnn_layer_kernel(tc, x, dist, w1, b1, w2, wh, bh, offs, out):
                 finish_d(t + 2)
             if 0 <= t - 1 < PIECES:
                 relu(t - 1)
-                mean_and_store(t - 1)
             if t < PIECES:
                 gather(t)
+            if 0 <= t - 2:
+                mean_and_store(t - 2)
             if t < PIECES:
                 project(t)

@@ -19,6 +19,7 @@ BLOCKS = C // P
 PIECE = 512
 PIECES = N // PIECE
 NODES = PIECE // A
+WARM_UP = 6
 
 FLOPS = 2 * M * C * N + 2 * M * C * S + 2 * M * N
 
@@ -76,6 +77,12 @@ def tile_pgnn_layer_kernel(tc, x, dist, w1, b1, w2, wh, bh, offs, out):
         nc.vector.tensor_scalar_mul(bh_quarter[:], bh_col[:], 0.25)
 
         x_bf = [held.tile([P, S], BF16, name=f"x_bf_{b}") for b in range(BLOCKS)]
+
+        zeros = held.tile([P, PIECE], BF16, name="zeros")
+        nc.gpsimd.memset(zeros[:], 0.0)
+        warm_ps = psum_z.tile([P, PIECE], F32, name="warm_ps", tag="z_ps")
+        for i in range(WARM_UP):
+            nc.tensor.matmul(warm_ps[:], zeros[:, 0:P], zeros[:], start=True, stop=True)
 
         dist_ps = {}
         d_ps = {}

@@ -19,7 +19,8 @@ BLOCKS = C // P
 PIECE = 512
 PIECES = N // PIECE
 NODES = PIECE // A
-WARM_UP = 6
+WARM_UP = 4
+DIST_ROWS = 4
 
 FLOPS = 2 * M * C * N + 2 * M * C * S + 2 * M * N
 
@@ -38,51 +39,62 @@ def tile_pgnn_layer_kernel(tc, x, dist, w1, b1, w2, wh, bh, offs, out):
         b1_col = held.tile([P, 1], F32, name="b1_col")
         w2_col = held.tile([P, 1], BF16, name="w2_col")
         bh_col = held.tile([P, 1], F32, name="bh_col")
-        dist_pad = held.tile([P, N], F32, name="dist_pad")
+        dist_rows = held.tile([P, (PIECES // DIST_ROWS) * PIECE], F32, name="dist_rows")
         wh_sb = held.tile([P, 2 * BLOCKS, M], BF16, name="wh_sb")
         offsets = held.tile([P, N // 16], U16, name="offsets")
         x_f32 = [held.tile([P, S], F32, name=f"x_f32_{b}") for b in range(BLOCKS)]
 
-        def piece(k):
-            return slice(k * PIECE, (k + 1) * PIECE)
+        def columns_of(k):
+            half = k // DIST_ROWS
+            return slice(half * PIECE, (half + 1) * PIECE)
 
         def load_dist(k):
-            nc.vector.memset(dist_pad[:, piece(k)], 0.0)
-            nc.scalar.dma_start(dist_pad[0:1, piece(k)], dist[:, piece(k)])
+            row = 32 * (k % DIST_ROWS)
+            nc.sync.dma_start(dist_rows[row : row + 1, columns_of(k)], dist[:, k * PIECE : (k + 1) * PIECE])
 
-        load_dist(0)
-        load_dist(1)
+        zeros = held.tile([P, P], BF16, name="zeros")
+        nc.vector.memset(zeros[:], 0.0)
         scratch = held.tile([P, 1], F32, name="scratch")
-        nc.gpsimd.memset(scratch[:], 0.0)
+        nc.vector.memset(scratch[:], 0.0)
         nc.scalar.activation(scratch[:], scratch[:], RELU)
-        for k in range(2, PIECES):
-            load_dist(k)
+        pick = held.tile([P, DIST_ROWS], F32, name="pick")
+        nc.vector.memset(pick[:], 0.0)
+        for q in range(DIST_ROWS):
+            nc.vector.memset(pick[32 * q : 32 * q + 1, q : q + 1], 1.0)
 
+        for half in range(PIECES // DIST_ROWS):
+            nc.gpsimd.memset(dist_rows[:, half * PIECE : (half + 1) * PIECE], 0.0)
         with nc.allow_non_contiguous_dma(reason="one element to a partition"):
             nc.sync.dma_start(w1_col[:], w1)
             nc.sync.dma_start(b1_col[:], b1)
+        for k in range(DIST_ROWS):
+            load_dist(k)
+        with nc.allow_non_contiguous_dma(reason="one element to a partition"):
             nc.sync.dma_start(w2_col[:], w2)
-            nc.sync.dma_start(bh_col[:], bh)
-        nc.sync.dma_start(offsets[:], offs)
         for b in range(BLOCKS):
             nc.sync.dma_start(x_f32[b][:], x[b * P : (b + 1) * P, :])
+        nc.sync.dma_start(offsets[:], offs)
+        for k in range(DIST_ROWS, PIECES):
+            load_dist(k)
         nc.sync.dma_start(wh_sb[:], wh.rearrange("(k p) m -> p k m", p=P))
+        with nc.allow_non_contiguous_dma(reason="one element to a partition"):
+            nc.sync.dma_start(bh_col[:], bh)
 
-        pick_row0 = held.tile([P, P], F32, name="pick_row0")
-        nc.gpsimd.memset(pick_row0[:], 0.0)
-        nc.gpsimd.memset(pick_row0[0:1, :], 1.0)
+        warm_ps = psum_z.tile([P, PIECE], F32, name="warm_ps", tag="z_ps")
+        for i in range(WARM_UP):
+            nc.tensor.matmul(
+                warm_ps[:].rearrange("p (n a) -> p n a", a=A),
+                zeros[:],
+                zeros[:].unsqueeze(2).to_broadcast([P, P, A]),
+                start=True,
+                stop=True,
+            )
         w2_wide = held.tile([P, M], BF16, name="w2_wide")
         nc.vector.tensor_copy(w2_wide[:], w2_col[:, 0:1].to_broadcast([P, M]))
         bh_quarter = held.tile([P, 1], F32, name="bh_quarter")
         nc.vector.tensor_scalar_mul(bh_quarter[:], bh_col[:], 0.25)
 
         x_bf = [held.tile([P, S], BF16, name=f"x_bf_{b}") for b in range(BLOCKS)]
-
-        zeros = held.tile([P, PIECE], BF16, name="zeros")
-        nc.gpsimd.memset(zeros[:], 0.0)
-        warm_ps = psum_z.tile([P, PIECE], F32, name="warm_ps", tag="z_ps")
-        for i in range(WARM_UP):
-            nc.tensor.matmul(warm_ps[:], zeros[:, 0:P], zeros[:], start=True, stop=True)
 
         dist_ps = {}
         d_ps = {}
@@ -92,7 +104,16 @@ def tile_pgnn_layer_kernel(tc, x, dist, w1, b1, w2, wh, bh, offs, out):
 
         def spread_dist(k):
             dist_ps[k] = psum_dist.tile([P, PIECE], F32, name="dist_ps")
-            nc.tensor.matmul(dist_ps[k][:], pick_row0[:], dist_pad[:, piece(k)], start=True, stop=True)
+            pick_row = pick[:, k % DIST_ROWS : k % DIST_ROWS + 1].to_broadcast([P, P])
+            first_column = columns_of(k).start
+            for j in range(0, PIECE, PIECE // 2):
+                nc.tensor.matmul(
+                    dist_ps[k][:, j : j + PIECE // 2],
+                    pick_row,
+                    dist_rows[:, first_column + j : first_column + j + PIECE // 2],
+                    start=True,
+                    stop=True,
+                )
 
         def start_d(k):
             hid = work.tile([P, PIECE], BF16, name="hid")
@@ -150,12 +171,12 @@ def tile_pgnn_layer_kernel(tc, x, dist, w1, b1, w2, wh, bh, offs, out):
         spread_dist(0)
         spread_dist(1)
         start_d(0)
+        finish_d(0)
         spread_dist(2)
         start_d(1)
-        finish_d(0)
+        finish_d(1)
         spread_dist(3)
         start_d(2)
-        finish_d(1)
         for b in range(BLOCKS):
             nc.vector.tensor_copy(x_bf[b][:], x_f32[b][:])
 

@@ -16,11 +16,13 @@ A = 4
 N = S * A
 M = 128
 BLOCKS = C // P
-PIECE = 512
-PIECES = N // PIECE
-NODES = PIECE // A
-WARM_UP = 4
+BANK = 512
+HALF = BANK // 2
+STARTS = [0, HALF] + list(range(BANK, N, BANK))
+WIDTHS = [HALF, HALF] + [BANK] * (N // BANK - 1)
+PIECES = len(STARTS)
 DIST_ROWS = 4
+WARM_UP = 4
 
 FLOPS = 2 * M * C * N + 2 * M * C * S + 2 * M * N
 
@@ -30,7 +32,7 @@ def tile_pgnn_layer_kernel(tc, x, dist, w1, b1, w2, wh, bh, offs, out):
     with (
         tc.tile_pool(name="held", bufs=1) as held,
         tc.tile_pool(name="work", bufs=3) as work,
-        tc.tile_pool(name="ahead", bufs=4) as ahead,
+        tc.tile_pool(name="whole", bufs=PIECES) as whole,
         tc.psum_pool(name="psum_dist", bufs=2) as psum_dist,
         tc.psum_pool(name="psum_d", bufs=2) as psum_d,
         tc.psum_pool(name="psum_z", bufs=3) as psum_z,
@@ -39,18 +41,18 @@ def tile_pgnn_layer_kernel(tc, x, dist, w1, b1, w2, wh, bh, offs, out):
         b1_col = held.tile([P, 1], F32, name="b1_col")
         w2_col = held.tile([P, 1], BF16, name="w2_col")
         bh_col = held.tile([P, 1], F32, name="bh_col")
-        dist_rows = held.tile([P, (PIECES // DIST_ROWS) * PIECE], F32, name="dist_rows")
+        dist_rows = held.tile([P, N // DIST_ROWS], F32, name="dist_rows")
         wh_sb = held.tile([P, 2 * BLOCKS, M], BF16, name="wh_sb")
         offsets = held.tile([P, N // 16], U16, name="offsets")
         x_f32 = [held.tile([P, S], F32, name=f"x_f32_{b}") for b in range(BLOCKS)]
+        x_bf = [held.tile([P, S], BF16, name=f"x_bf_{b}") for b in range(BLOCKS)]
 
-        def columns_of(k):
-            half = k // DIST_ROWS
-            return slice(half * PIECE, (half + 1) * PIECE)
-
-        def load_dist(k):
-            row = 32 * (k % DIST_ROWS)
-            nc.sync.dma_start(dist_rows[row : row + 1, columns_of(k)], dist[:, k * PIECE : (k + 1) * PIECE])
+        def load_dist(bank):
+            row = 32 * (bank % DIST_ROWS)
+            column = (bank // DIST_ROWS) * BANK
+            nc.sync.dma_start(
+                dist_rows[row : row + 1, column : column + BANK], dist[:, bank * BANK : (bank + 1) * BANK]
+            )
 
         zeros = held.tile([P, P], BF16, name="zeros")
         nc.vector.memset(zeros[:], 0.0)
@@ -62,25 +64,25 @@ def tile_pgnn_layer_kernel(tc, x, dist, w1, b1, w2, wh, bh, offs, out):
         for q in range(DIST_ROWS):
             nc.vector.memset(pick[32 * q : 32 * q + 1, q : q + 1], 1.0)
 
-        for half in range(PIECES // DIST_ROWS):
-            nc.gpsimd.memset(dist_rows[:, half * PIECE : (half + 1) * PIECE], 0.0)
+        for column in range(0, N // DIST_ROWS, BANK):
+            nc.gpsimd.memset(dist_rows[:, column : column + BANK], 0.0)
         with nc.allow_non_contiguous_dma(reason="one element to a partition"):
             nc.sync.dma_start(w1_col[:], w1)
             nc.sync.dma_start(b1_col[:], b1)
-        for k in range(DIST_ROWS):
-            load_dist(k)
+        for bank in range(DIST_ROWS):
+            load_dist(bank)
         with nc.allow_non_contiguous_dma(reason="one element to a partition"):
             nc.sync.dma_start(w2_col[:], w2)
         for b in range(BLOCKS):
             nc.sync.dma_start(x_f32[b][:], x[b * P : (b + 1) * P, :])
         nc.sync.dma_start(offsets[:], offs)
-        for k in range(DIST_ROWS, PIECES):
-            load_dist(k)
+        for bank in range(DIST_ROWS, N // BANK):
+            load_dist(bank)
         nc.sync.dma_start(wh_sb[:], wh.rearrange("(k p) m -> p k m", p=P))
         with nc.allow_non_contiguous_dma(reason="one element to a partition"):
             nc.sync.dma_start(bh_col[:], bh)
 
-        warm_ps = psum_z.tile([P, PIECE], F32, name="warm_ps", tag="z_ps")
+        warm_ps = psum_z.tile([P, BANK], F32, name="warm_ps", tag="z_ps")
         for i in range(WARM_UP):
             nc.tensor.matmul(
                 warm_ps[:].rearrange("p (n a) -> p n a", a=A),
@@ -94,104 +96,107 @@ def tile_pgnn_layer_kernel(tc, x, dist, w1, b1, w2, wh, bh, offs, out):
         bh_quarter = held.tile([P, 1], F32, name="bh_quarter")
         nc.vector.tensor_scalar_mul(bh_quarter[:], bh_col[:], 0.25)
 
-        x_bf = [held.tile([P, S], BF16, name=f"x_bf_{b}") for b in range(BLOCKS)]
-
         dist_ps = {}
         d_ps = {}
         d_sb = {}
+        msg = {}
         z_ps = {}
         h = {}
 
         def spread_dist(k):
-            dist_ps[k] = psum_dist.tile([P, PIECE], F32, name="dist_ps")
-            pick_row = pick[:, k % DIST_ROWS : k % DIST_ROWS + 1].to_broadcast([P, P])
-            first_column = columns_of(k).start
-            for j in range(0, PIECE, PIECE // 2):
+            bank = STARTS[k] // BANK
+            pick_row = pick[:, bank % DIST_ROWS : bank % DIST_ROWS + 1].to_broadcast([P, P])
+            first_column = (bank // DIST_ROWS) * BANK + STARTS[k] % BANK
+            dist_ps[k] = psum_dist.tile([P, BANK], F32, name="dist_ps")
+            for j in range(0, WIDTHS[k], HALF):
                 nc.tensor.matmul(
-                    dist_ps[k][:, j : j + PIECE // 2],
+                    dist_ps[k][:, j : j + HALF],
                     pick_row,
-                    dist_rows[:, first_column + j : first_column + j + PIECE // 2],
+                    dist_rows[:, first_column + j : first_column + j + HALF],
                     start=True,
                     stop=True,
                 )
 
         def start_d(k):
-            hid = work.tile([P, PIECE], BF16, name="hid")
+            width = WIDTHS[k]
+            hid = work.tile([P, BANK], BF16, name="hid")
             nc.scalar.activation(
-                hid[:], dist_ps[k][:], RELU, bias=b1_col[:, 0:1], scale=w1_col[:, 0:1]
+                hid[:, 0:width], dist_ps[k][:, 0:width], RELU, bias=b1_col[:, 0:1], scale=w1_col[:, 0:1]
             )
-            d_ps[k] = psum_d.tile([P, PIECE], F32, name="d_ps")
-            nc.tensor.matmul(d_ps[k][:], w2_wide[:], hid[:], start=True, stop=True)
+            d_ps[k] = psum_d.tile([P, BANK], F32, name="d_ps")
+            nc.tensor.matmul(d_ps[k][:, 0:width], w2_wide[:], hid[:, 0:width], start=True, stop=True)
 
         def finish_d(k):
-            d_sb[k] = ahead.tile([P, PIECE], F32, name="d_sb")
-            nc.scalar.activation(d_sb[k][:], d_ps[k][:], COPY, bias=0.25)
-
-        msg = {}
+            width = WIDTHS[k]
+            d_sb[k] = whole.tile([P, BANK], F32, name="d_sb")
+            nc.scalar.activation(d_sb[k][:, 0:width], d_ps[k][:, 0:width], COPY, bias=0.25)
 
         def gather(k):
-            piece_offsets = offsets[:, k * (PIECE // 16) : (k + 1) * (PIECE // 16)]
-            msg[k] = [work.tile([P, PIECE], F32, name=f"msg{b}") for b in range(BLOCKS)]
+            width = WIDTHS[k]
+            piece_offsets = offsets[:, STARTS[k] // 16 : (STARTS[k] + width) // 16]
+            msg[k] = [whole.tile([P, BANK], F32, name=f"msg{b}") for b in range(BLOCKS)]
             for b in range(BLOCKS):
                 nc.vector.tensor_tensor(
-                    msg[k][b][:], x_f32[b][:].indirect(piece_offsets), d_sb[k][:], MULT
+                    msg[k][b][:, 0:width], x_f32[b][:].indirect(piece_offsets), d_sb[k][:, 0:width], MULT
                 )
 
         def project(k):
-            msg_bf = [work.tile([P, PIECE], BF16, name=f"msg_bf{b}") for b in range(BLOCKS)]
+            width = WIDTHS[k]
+            msg_bf = [work.tile([P, BANK], BF16, name=f"msg_bf{b}") for b in range(BLOCKS)]
             for b in range(BLOCKS):
-                nc.scalar.activation(msg_bf[b][:], msg[k][b][:], COPY)
-            z_ps[k] = psum_z.tile([P, PIECE], F32, name="z_ps")
-            z_by_node = z_ps[k][:].rearrange("p (n a) -> p n a", a=A)
+                nc.scalar.activation(msg_bf[b][:, 0:width], msg[k][b][:, 0:width], COPY)
+            z_ps[k] = psum_z.tile([P, BANK], F32, name="z_ps")
+            z_by_node = z_ps[k][:, 0:width].rearrange("p (n a) -> p n a", a=A)
             for b in range(BLOCKS):
-                own = x_bf[b][:, k * NODES : (k + 1) * NODES]
+                own = x_bf[b][:, STARTS[k] // A : (STARTS[k] + width) // A]
                 nc.tensor.matmul(
                     z_by_node,
                     wh_sb[:, BLOCKS + b, :],
-                    own.unsqueeze(2).to_broadcast([P, NODES, A]),
+                    own.unsqueeze(2).to_broadcast([P, width // A, A]),
                     start=(b == 0),
                     stop=False,
                 )
             for b in range(BLOCKS):
                 nc.tensor.matmul(
-                    z_ps[k][:], wh_sb[:, b, :], msg_bf[b][:], start=False, stop=(b == BLOCKS - 1)
+                    z_ps[k][:, 0:width],
+                    wh_sb[:, b, :],
+                    msg_bf[b][:, 0:width],
+                    start=False,
+                    stop=(b == BLOCKS - 1),
                 )
 
         def relu(k):
-            h[k] = work.tile([P, PIECE], F32, name="h")
-            nc.scalar.activation(h[k][:], z_ps[k][:], RELU, bias=bh_quarter[:, 0:1], scale=0.25)
+            width = WIDTHS[k]
+            h[k] = whole.tile([P, BANK], F32, name="h")
+            nc.scalar.activation(
+                h[k][:, 0:width], z_ps[k][:, 0:width], RELU, bias=bh_quarter[:, 0:1], scale=0.25
+            )
 
         def mean_and_store(k):
-            mean = work.tile([P, NODES], F32, name="mean")
+            width = WIDTHS[k]
+            mean = work.tile([P, BANK // A], F32, name="mean")
             nc.vector.tensor_reduce(
-                mean[:], h[k][:].rearrange("p (n a) -> p n a", a=A), axis=X_AXIS, op=ADD
+                mean[:, 0 : width // A],
+                h[k][:, 0:width].rearrange("p (n a) -> p n a", a=A),
+                axis=X_AXIS,
+                op=ADD,
             )
-            nc.sync.dma_start(out[:, k * NODES : (k + 1) * NODES], mean[:])
+            nc.sync.dma_start(out[:, STARTS[k] // A : (STARTS[k] + width) // A], mean[:, 0 : width // A])
 
         spread_dist(0)
-        spread_dist(1)
-        start_d(0)
-        finish_d(0)
-        spread_dist(2)
-        start_d(1)
-        finish_d(1)
-        spread_dist(3)
-        start_d(2)
+        for k in range(PIECES):
+            if k + 1 < PIECES:
+                spread_dist(k + 1)
+            start_d(k)
+            finish_d(k)
         for b in range(BLOCKS):
             nc.vector.tensor_copy(x_bf[b][:], x_f32[b][:])
 
-        for t in range(PIECES + 2):
-            if t + 4 < PIECES:
-                spread_dist(t + 4)
-            if t + 3 < PIECES:
-                start_d(t + 3)
-            if t + 2 < PIECES:
-                finish_d(t + 2)
-            if 0 <= t - 1 < PIECES:
+        for t in range(PIECES + 1):
+            if 0 <= t - 1:
                 relu(t - 1)
             if t < PIECES:
                 gather(t)
-            if 0 <= t - 2:
-                mean_and_store(t - 2)
-            if t < PIECES:
                 project(t)
+        for k in range(PIECES):
+            mean_and_store(k)

@@ -47,11 +47,12 @@ def tile_pgnn_layer_kernel(tc, x, dist, w1, b1, w2, wh, bh, offs, out):
         x_f32 = [held.tile([P, S], F32, name=f"x_f32_{b}") for b in range(BLOCKS)]
         x_bf = [held.tile([P, S], BF16, name=f"x_bf_{b}") for b in range(BLOCKS)]
 
-        def load_dist(bank):
-            row = 32 * (bank % DIST_ROWS)
-            column = (bank // DIST_ROWS) * BANK
+        def load_dist(half):
+            every_32nd_row = dist_rows[:].rearrange("(q r) j -> q r j", r=P // DIST_ROWS)[:, 0, :]
+            first = half * DIST_ROWS * BANK
             nc.sync.dma_start(
-                dist_rows[row : row + 1, column : column + BANK], dist[:, bank * BANK : (bank + 1) * BANK]
+                every_32nd_row[:, half * BANK : (half + 1) * BANK],
+                dist[:, first : first + DIST_ROWS * BANK].rearrange("o (q j) -> (o q) j", q=DIST_ROWS),
             )
 
         zeros = held.tile([P, P], BF16, name="zeros")
@@ -69,15 +70,13 @@ def tile_pgnn_layer_kernel(tc, x, dist, w1, b1, w2, wh, bh, offs, out):
         with nc.allow_non_contiguous_dma(reason="one element to a partition"):
             nc.sync.dma_start(w1_col[:], w1)
             nc.sync.dma_start(b1_col[:], b1)
-        for bank in range(DIST_ROWS):
-            load_dist(bank)
+        load_dist(0)
         with nc.allow_non_contiguous_dma(reason="one element to a partition"):
             nc.sync.dma_start(w2_col[:], w2)
         for b in range(BLOCKS):
             nc.sync.dma_start(x_f32[b][:], x[b * P : (b + 1) * P, :])
         nc.sync.dma_start(offsets[:], offs)
-        for bank in range(DIST_ROWS, N // BANK):
-            load_dist(bank)
+        load_dist(1)
         nc.sync.dma_start(wh_sb[:], wh.rearrange("(k p) m -> p k m", p=P))
         with nc.allow_non_contiguous_dma(reason="one element to a partition"):
             nc.sync.dma_start(bh_col[:], bh)

@@ -23,6 +23,7 @@ WIDTHS = [HALF, HALF] + [BANK] * (N // BANK - 1)
 PIECES = len(STARTS)
 DIST_ROWS = 4
 WARM_UP = 4
+MEAN_ENTRIES = 2 * BANK
 
 FLOPS = 2 * M * C * N + 2 * M * C * S + 2 * M * N
 
@@ -46,6 +47,8 @@ def tile_pgnn_layer_kernel(tc, x, dist, w1, b1, w2, wh, bh, offs, out):
         offsets = held.tile([P, N // 16], U16, name="offsets")
         x_f32 = [held.tile([P, S], F32, name=f"x_f32_{b}") for b in range(BLOCKS)]
         x_bf = [held.tile([P, S], BF16, name=f"x_bf_{b}") for b in range(BLOCKS)]
+        h = held.tile([P, N], F32, name="h")
+        mean = held.tile([P, S], F32, name="mean")
 
         def load_dist(half):
             every_32nd_row = dist_rows[:].rearrange("(q r) j -> q r j", r=P // DIST_ROWS)[:, 0, :]
@@ -100,7 +103,6 @@ def tile_pgnn_layer_kernel(tc, x, dist, w1, b1, w2, wh, bh, offs, out):
         d_sb = {}
         msg = {}
         z_ps = {}
-        h = {}
 
         def spread_dist(k):
             bank = STARTS[k] // BANK
@@ -166,21 +168,23 @@ def tile_pgnn_layer_kernel(tc, x, dist, w1, b1, w2, wh, bh, offs, out):
 
         def relu(k):
             width = WIDTHS[k]
-            h[k] = whole.tile([P, BANK], F32, name="h")
             nc.scalar.activation(
-                h[k][:, 0:width], z_ps[k][:, 0:width], RELU, bias=bh_quarter[:, 0:1], scale=0.25
+                h[:, STARTS[k] : STARTS[k] + width],
+                z_ps[k][:, 0:width],
+                RELU,
+                bias=bh_quarter[:, 0:1],
+                scale=0.25,
             )
 
-        def mean_and_store(k):
-            width = WIDTHS[k]
-            mean = work.tile([P, BANK // A], F32, name="mean")
+        def mean_and_store(first):
+            nodes = slice(first // A, (first + MEAN_ENTRIES) // A)
             nc.vector.tensor_reduce(
-                mean[:, 0 : width // A],
-                h[k][:, 0:width].rearrange("p (n a) -> p n a", a=A),
+                mean[:, nodes],
+                h[:, first : first + MEAN_ENTRIES].rearrange("p (n a) -> p n a", a=A),
                 axis=X_AXIS,
                 op=ADD,
             )
-            nc.sync.dma_start(out[:, STARTS[k] // A : (STARTS[k] + width) // A], mean[:, 0 : width // A])
+            nc.sync.dma_start(out[:, nodes], mean[:, nodes])
 
         spread_dist(0)
         for k in range(PIECES):
@@ -197,5 +201,5 @@ def tile_pgnn_layer_kernel(tc, x, dist, w1, b1, w2, wh, bh, offs, out):
             if t < PIECES:
                 gather(t)
                 project(t)
-        for k in range(PIECES):
-            mean_and_store(k)
+        for first in range(0, N, MEAN_ENTRIES):
+            mean_and_store(first)

@@ -22,7 +22,6 @@ STARTS = [0, HALF] + list(range(BANK, N, BANK))
 WIDTHS = [HALF, HALF] + [BANK] * (N // BANK - 1)
 PIECES = len(STARTS)
 DIST_ROWS = 4
-WARM_UP = 4
 MEAN_ENTRIES = 2 * BANK
 
 FLOPS = 2 * M * C * N + 2 * M * C * S + 2 * M * N
@@ -58,8 +57,6 @@ def tile_pgnn_layer_kernel(tc, x, dist, w1, b1, w2, wh, bh, offs, out):
                 dist[:, first : first + DIST_ROWS * BANK].rearrange("o (q j) -> (o q) j", q=DIST_ROWS),
             )
 
-        zeros = held.tile([P, P], BF16, name="zeros")
-        nc.vector.memset(zeros[:], 0.0)
         scratch = held.tile([P, 1], F32, name="scratch")
         nc.vector.memset(scratch[:], 0.0)
         nc.scalar.activation(scratch[:], scratch[:], RELU)
@@ -84,15 +81,6 @@ def tile_pgnn_layer_kernel(tc, x, dist, w1, b1, w2, wh, bh, offs, out):
         with nc.allow_non_contiguous_dma(reason="one element to a partition"):
             nc.sync.dma_start(bh_col[:], bh)
 
-        warm_ps = psum_z.tile([P, BANK], F32, name="warm_ps", tag="z_ps")
-        for i in range(WARM_UP):
-            nc.tensor.matmul(
-                warm_ps[:].rearrange("p (n a) -> p n a", a=A),
-                zeros[:],
-                zeros[:].unsqueeze(2).to_broadcast([P, P, A]),
-                start=True,
-                stop=True,
-            )
         w2_wide = held.tile([P, M], BF16, name="w2_wide")
         nc.vector.tensor_copy(w2_wide[:], w2_col[:, 0:1].to_broadcast([P, M]))
         bh_quarter = held.tile([P, 1], F32, name="bh_quarter")

@@ -7,7 +7,6 @@ RELU = mybir.ActivationFunctionType.Relu
 COPY = mybir.ActivationFunctionType.Copy
 MULT = mybir.AluOpType.mult
 ADD = mybir.AluOpType.add
-X_AXIS = mybir.AxisListType.X
 
 P = 128
 C = 256
@@ -18,11 +17,11 @@ M = 128
 BLOCKS = C // P
 BANK = 512
 HALF = BANK // 2
-STARTS = [0, HALF] + list(range(BANK, N, BANK))
-WIDTHS = [HALF, HALF] + [BANK] * (N // BANK - 1)
+WIDTHS = [HALF, HALF] + [BANK] * (N // BANK - 2) + [HALF, HALF]
+STARTS = [sum(WIDTHS[:k]) for k in range(len(WIDTHS))]
 PIECES = len(STARTS)
 DIST_ROWS = 4
-MEAN_ENTRIES = 2 * BANK
+SUMS = [2 * BANK] * (N // BANK // 2 - 1) + [BANK, HALF, HALF]
 
 FLOPS = 2 * M * C * N + 2 * M * C * S + 2 * M * N
 
@@ -164,14 +163,13 @@ def tile_pgnn_layer_kernel(tc, x, dist, w1, b1, w2, wh, bh, offs, out):
                 scale=0.25,
             )
 
-        def mean_and_store(first):
-            nodes = slice(first // A, (first + MEAN_ENTRIES) // A)
-            nc.vector.tensor_reduce(
-                mean[:, nodes],
-                h[:, first : first + MEAN_ENTRIES].rearrange("p (n a) -> p n a", a=A),
-                axis=X_AXIS,
-                op=ADD,
-            )
+        def mean_and_store(first, entries):
+            nodes = slice(first // A, (first + entries) // A)
+            h_by_node = h[:, first : first + entries].rearrange("p (n a) -> p n a", a=A)
+            pairs = work.tile([P, max(SUMS) // A, 2], F32, name="pairs")
+            pairs_here = pairs[:, 0 : entries // A, :]
+            nc.vector.tensor_tensor(pairs_here, h_by_node[:, :, 0:2], h_by_node[:, :, 2:4], ADD)
+            nc.vector.tensor_tensor(mean[:, nodes], pairs_here[:, :, 0], pairs_here[:, :, 1], ADD)
             nc.sync.dma_start(out[:, nodes], mean[:, nodes])
 
         spread_dist(0)
@@ -189,5 +187,5 @@ def tile_pgnn_layer_kernel(tc, x, dist, w1, b1, w2, wh, bh, offs, out):
             if t < PIECES:
                 gather(t)
                 project(t)
-        for first in range(0, N, MEAN_ENTRIES):
-            mean_and_store(first)
+        for s, entries in enumerate(SUMS):
+            mean_and_store(sum(SUMS[:s]), entries)

@@ -1,4 +1,5 @@
 import concourse.mybir as mybir
+from concourse.masks import make_identity
 
 F32 = mybir.dt.float32
 BF16 = mybir.dt.bfloat16
@@ -21,7 +22,14 @@ WIDTHS = [HALF, HALF] + [BANK] * (N // BANK - 2) + [HALF, HALF]
 STARTS = [sum(WIDTHS[:k]) for k in range(len(WIDTHS))]
 PIECES = len(STARTS)
 DIST_ROWS = 4
-SUMS = [2 * BANK] * (N // BANK // 2 - 1) + [BANK, HALF, HALF]
+TENSOR_SUMS = [2, 3]
+VECTOR_SUMS = [
+    (0, BANK),
+    (3 * BANK, 3 * BANK),
+    (6 * BANK, BANK),
+    (7 * BANK, HALF),
+    (7 * BANK + HALF, HALF),
+]
 
 FLOPS = 2 * M * C * N + 2 * M * C * S + 2 * M * N
 
@@ -35,6 +43,7 @@ def tile_pgnn_layer_kernel(tc, x, dist, w1, b1, w2, wh, bh, offs, out):
         tc.psum_pool(name="psum_dist", bufs=2) as psum_dist,
         tc.psum_pool(name="psum_d", bufs=2) as psum_d,
         tc.psum_pool(name="psum_z", bufs=3) as psum_z,
+        tc.psum_pool(name="psum_mean", bufs=1) as psum_mean,
     ):
         w1_col = held.tile([P, 1], F32, name="w1_col")
         b1_col = held.tile([P, 1], F32, name="b1_col")
@@ -59,6 +68,7 @@ def tile_pgnn_layer_kernel(tc, x, dist, w1, b1, w2, wh, bh, offs, out):
         scratch = held.tile([P, 1], F32, name="scratch")
         nc.vector.memset(scratch[:], 0.0)
         nc.scalar.activation(scratch[:], scratch[:], RELU)
+        identity = held.tile([P, P], F32, name="identity")
         pick = held.tile([P, DIST_ROWS], F32, name="pick")
         nc.vector.memset(pick[:], 0.0)
         for q in range(DIST_ROWS):
@@ -66,6 +76,7 @@ def tile_pgnn_layer_kernel(tc, x, dist, w1, b1, w2, wh, bh, offs, out):
 
         for column in range(0, N // DIST_ROWS, BANK):
             nc.gpsimd.memset(dist_rows[:, column : column + BANK], 0.0)
+        make_identity(nc, identity[:])
         with nc.allow_non_contiguous_dma(reason="one element to a partition"):
             nc.sync.dma_start(w1_col[:], w1)
             nc.sync.dma_start(b1_col[:], b1)
@@ -155,18 +166,33 @@ def tile_pgnn_layer_kernel(tc, x, dist, w1, b1, w2, wh, bh, offs, out):
 
         def relu(k):
             width = WIDTHS[k]
-            nc.scalar.activation(
-                h[:, STARTS[k] : STARTS[k] + width],
-                z_ps[k][:, 0:width],
-                RELU,
-                bias=bh_quarter[:, 0:1],
-                scale=0.25,
-            )
+            h_here = h[:, STARTS[k] : STARTS[k] + width]
+            z_here = z_ps[k][:, 0:width]
+            if k in TENSOR_SUMS:
+                h_here = h_here.rearrange("p (a n) -> p n a", a=A)
+                z_here = z_here.rearrange("p (n a) -> p n a", a=A)
+            nc.scalar.activation(h_here, z_here, RELU, bias=bh_quarter[:, 0:1], scale=0.25)
+
+        def tensor_sums():
+            mean_ps = psum_mean.tile([P, BANK], F32, name="mean_ps")
+            nodes = BANK // A
+            for i, k in enumerate(TENSOR_SUMS):
+                for a in range(A):
+                    nc.tensor.matmul(
+                        mean_ps[:, i * nodes : (i + 1) * nodes],
+                        identity[:],
+                        h[:, STARTS[k] + a * nodes : STARTS[k] + (a + 1) * nodes],
+                        start=(a == 0),
+                        stop=(a == A - 1),
+                    )
+            taken = slice(STARTS[TENSOR_SUMS[0]] // A, STARTS[TENSOR_SUMS[-1]] // A + nodes)
+            nc.scalar.copy(mean[:, taken], mean_ps[:, 0 : len(TENSOR_SUMS) * nodes])
+            nc.sync.dma_start(out[:, taken], mean[:, taken])
 
         def mean_and_store(first, entries):
             nodes = slice(first // A, (first + entries) // A)
             h_by_node = h[:, first : first + entries].rearrange("p (n a) -> p n a", a=A)
-            pairs = work.tile([P, max(SUMS) // A, 2], F32, name="pairs")
+            pairs = work.tile([P, 3 * BANK // A, 2], F32, name="pairs")
             pairs_here = pairs[:, 0 : entries // A, :]
             nc.vector.tensor_tensor(pairs_here, h_by_node[:, :, 0:2], h_by_node[:, :, 2:4], ADD)
             nc.vector.tensor_tensor(mean[:, nodes], pairs_here[:, :, 0], pairs_here[:, :, 1], ADD)
@@ -187,5 +213,7 @@ def tile_pgnn_layer_kernel(tc, x, dist, w1, b1, w2, wh, bh, offs, out):
             if t < PIECES:
                 gather(t)
                 project(t)
-        for s, entries in enumerate(SUMS):
-            mean_and_store(sum(SUMS[:s]), entries)
+            if t - 1 == TENSOR_SUMS[-1]:
+                tensor_sums()
+        for first, entries in VECTOR_SUMS:
+            mean_and_store(first, entries)

@@ -143,7 +143,10 @@ def tile_pgnn_layer_kernel(tc, x, dist, w1, b1, w2, wh, bh, offs, out):
             width = WIDTHS[k]
             msg_bf = [work.tile([P, BANK], BF16, name=f"msg_bf{b}") for b in range(BLOCKS)]
             for b in range(BLOCKS):
-                nc.scalar.activation(msg_bf[b][:, 0:width], msg[k][b][:, 0:width], COPY)
+                if STARTS[k] >= N - BANK:
+                    nc.vector.tensor_copy(msg_bf[b][:, 0:width], msg[k][b][:, 0:width])
+                else:
+                    nc.scalar.activation(msg_bf[b][:, 0:width], msg[k][b][:, 0:width], COPY)
             z_ps[k] = psum_z.tile([P, BANK], F32, name="z_ps")
             z_by_node = z_ps[k][:, 0:width].rearrange("p (n a) -> p n a", a=A)
             for b in range(BLOCKS):

@@ -21,7 +21,6 @@ HALF = BANK // 2
 WIDTHS = [HALF, HALF] + [BANK] * (N // BANK - 2) + [HALF, HALF]
 STARTS = [sum(WIDTHS[:k]) for k in range(len(WIDTHS))]
 PIECES = len(STARTS)
-DIST_ROWS = 4
 TENSOR_SUMS = [2, 3]
 VECTOR_SUMS = [
     (0, BANK),
@@ -38,7 +37,9 @@ def tile_pgnn_layer_kernel(tc, x, dist, w1, b1, w2, wh, bh, offs, out):
     nc = tc.nc
     with (
         tc.tile_pool(name="held", bufs=1) as held,
+        tc.tile_pool(name="early", bufs=1) as early,
         tc.tile_pool(name="work", bufs=3) as work,
+        tc.tile_pool(name="last_rounded", bufs=2) as last_rounded,
         tc.tile_pool(name="whole", bufs=PIECES) as whole,
         tc.psum_pool(name="psum_dist", bufs=2) as psum_dist,
         tc.psum_pool(name="psum_d", bufs=2) as psum_d,
@@ -49,45 +50,30 @@ def tile_pgnn_layer_kernel(tc, x, dist, w1, b1, w2, wh, bh, offs, out):
         b1_col = held.tile([P, 1], F32, name="b1_col")
         w2_col = held.tile([P, 1], BF16, name="w2_col")
         bh_col = held.tile([P, 1], F32, name="bh_col")
-        dist_rows = held.tile([P, N // DIST_ROWS], F32, name="dist_rows")
-        wh_sb = held.tile([P, 2 * BLOCKS, M], BF16, name="wh_sb")
+        dist_rows = early.tile([P, P], F32, name="dist_rows", tag="early")
+        dist_columns = held.tile([P, N // P], F32, name="dist_columns")
         offsets = held.tile([P, N // 16], U16, name="offsets")
         x_f32 = [held.tile([P, S], F32, name=f"x_f32_{b}") for b in range(BLOCKS)]
         x_bf = [held.tile([P, S], BF16, name=f"x_bf_{b}") for b in range(BLOCKS)]
         h = held.tile([P, N], F32, name="h")
         mean = held.tile([P, S], F32, name="mean")
 
-        def load_dist(half):
-            every_32nd_row = dist_rows[:].rearrange("(q r) j -> q r j", r=P // DIST_ROWS)[:, 0, :]
-            first = half * DIST_ROWS * BANK
-            nc.sync.dma_start(
-                every_32nd_row[:, half * BANK : (half + 1) * BANK],
-                dist[:, first : first + DIST_ROWS * BANK].rearrange("o (q j) -> (o q) j", q=DIST_ROWS),
-            )
-
         scratch = held.tile([P, 1], F32, name="scratch")
         nc.vector.memset(scratch[:], 0.0)
         nc.scalar.activation(scratch[:], scratch[:], RELU)
         identity = held.tile([P, P], F32, name="identity")
-        pick = held.tile([P, DIST_ROWS], F32, name="pick")
-        nc.vector.memset(pick[:], 0.0)
-        for q in range(DIST_ROWS):
-            nc.vector.memset(pick[32 * q : 32 * q + 1, q : q + 1], 1.0)
 
-        for column in range(0, N // DIST_ROWS, BANK):
-            nc.gpsimd.memset(dist_rows[:, column : column + BANK], 0.0)
+        nc.gpsimd.memset(dist_rows[:], 0.0)
         make_identity(nc, identity[:])
         with nc.allow_non_contiguous_dma(reason="one element to a partition"):
             nc.sync.dma_start(w1_col[:], w1)
             nc.sync.dma_start(b1_col[:], b1)
-        load_dist(0)
+        nc.sync.dma_start(dist_rows[0 : N // P, :], dist.rearrange("o (q j) -> (o q) j", j=P))
         with nc.allow_non_contiguous_dma(reason="one element to a partition"):
             nc.sync.dma_start(w2_col[:], w2)
         for b in range(BLOCKS):
             nc.sync.dma_start(x_f32[b][:], x[b * P : (b + 1) * P, :])
         nc.sync.dma_start(offsets[:], offs)
-        load_dist(1)
-        nc.sync.dma_start(wh_sb[:], wh.rearrange("(k p) m -> p k m", p=P))
         with nc.allow_non_contiguous_dma(reason="one element to a partition"):
             nc.sync.dma_start(bh_col[:], bh)
 
@@ -102,18 +88,19 @@ def tile_pgnn_layer_kernel(tc, x, dist, w1, b1, w2, wh, bh, offs, out):
         msg = {}
         z_ps = {}
 
+        def turn_dist():
+            turned = psum_dist.tile([P, BANK], F32, name="dist_ps")
+            nc.tensor.transpose(turned[:, 0:P], dist_rows[:], identity[:])
+            nc.scalar.copy(dist_columns[:], turned[:, 0 : N // P])
+
         def spread_dist(k):
-            bank = STARTS[k] // BANK
-            pick_row = pick[:, bank % DIST_ROWS : bank % DIST_ROWS + 1].to_broadcast([P, P])
-            first_column = (bank // DIST_ROWS) * BANK + STARTS[k] % BANK
             dist_ps[k] = psum_dist.tile([P, BANK], F32, name="dist_ps")
-            for j in range(0, WIDTHS[k], HALF):
-                nc.tensor.matmul(
-                    dist_ps[k][:, j : j + HALF],
-                    pick_row,
-                    dist_rows[:, first_column + j : first_column + j + HALF],
-                    start=True,
-                    stop=True,
+            for j in range(0, WIDTHS[k], P):
+                q = (STARTS[k] + j) // P
+                nc.tensor.transpose(
+                    dist_ps[k][:, j : j + P],
+                    dist_columns[:, q : q + 1].to_broadcast([P, P]),
+                    identity[:],
                 )
 
         def start_d(k):
@@ -141,9 +128,11 @@ def tile_pgnn_layer_kernel(tc, x, dist, w1, b1, w2, wh, bh, offs, out):
 
         def project(k):
             width = WIDTHS[k]
-            msg_bf = [work.tile([P, BANK], BF16, name=f"msg_bf{b}") for b in range(BLOCKS)]
+            last_bank = STARTS[k] >= N - BANK
+            rounded = last_rounded if last_bank else work
+            msg_bf = [rounded.tile([P, BANK], BF16, name=f"msg_bf{b}") for b in range(BLOCKS)]
             for b in range(BLOCKS):
-                if STARTS[k] >= N - BANK:
+                if last_bank:
                     nc.vector.tensor_copy(msg_bf[b][:, 0:width], msg[k][b][:, 0:width])
                 else:
                     nc.scalar.activation(msg_bf[b][:, 0:width], msg[k][b][:, 0:width], COPY)
@@ -201,6 +190,9 @@ def tile_pgnn_layer_kernel(tc, x, dist, w1, b1, w2, wh, bh, offs, out):
             nc.vector.tensor_tensor(mean[:, nodes], pairs_here[:, :, 0], pairs_here[:, :, 1], ADD)
             nc.sync.dma_start(out[:, nodes], mean[:, nodes])
 
+        turn_dist()
+        wh_sb = early.tile([P, 2 * BLOCKS, M], BF16, name="wh_sb", tag="early")
+        nc.sync.dma_start(wh_sb[:], wh.rearrange("(k p) m -> p k m", p=P))
         spread_dist(0)
         for k in range(PIECES):
             if k + 1 < PIECES:

@@ -1,5 +1,4 @@
 import concourse.mybir as mybir
-from concourse.masks import make_identity
 
 F32 = mybir.dt.float32
 BF16 = mybir.dt.bfloat16
@@ -7,9 +6,11 @@ U16 = mybir.dt.uint16
 RELU = mybir.ActivationFunctionType.Relu
 COPY = mybir.ActivationFunctionType.Copy
 MULT = mybir.AluOpType.mult
+IS_EQUAL = mybir.AluOpType.is_equal
 ADD = mybir.AluOpType.add
 
 P = 128
+QUADRANT = 32
 C = 256
 S = 1024
 A = 4
@@ -21,9 +22,8 @@ HALF = BANK // 2
 WIDTHS = [HALF, HALF] + [BANK] * (N // BANK - 2) + [HALF, HALF]
 STARTS = [sum(WIDTHS[:k]) for k in range(len(WIDTHS))]
 PIECES = len(STARTS)
-TENSOR_SUMS = [2, 3]
+TENSOR_SUMS = 3 * BANK
 VECTOR_SUMS = [
-    (0, BANK),
     (3 * BANK, 3 * BANK),
     (6 * BANK, BANK),
     (7 * BANK, HALF),
@@ -37,7 +37,6 @@ def tile_pgnn_layer_kernel(tc, x, dist, w1, b1, w2, wh, bh, offs, out):
     nc = tc.nc
     with (
         tc.tile_pool(name="held", bufs=1) as held,
-        tc.tile_pool(name="early", bufs=1) as early,
         tc.tile_pool(name="work", bufs=3) as work,
         tc.tile_pool(name="last_rounded", bufs=2) as last_rounded,
         tc.tile_pool(name="whole", bufs=PIECES) as whole,
@@ -50,7 +49,8 @@ def tile_pgnn_layer_kernel(tc, x, dist, w1, b1, w2, wh, bh, offs, out):
         b1_col = held.tile([P, 1], F32, name="b1_col")
         w2_col = held.tile([P, 1], BF16, name="w2_col")
         bh_col = held.tile([P, 1], F32, name="bh_col")
-        dist_rows = early.tile([P, P], F32, name="dist_rows", tag="early")
+        dist_rows = held.tile([P, P], F32, name="dist_rows")
+        wh_sb = held.tile([P, 2 * BLOCKS, M], BF16, name="wh_sb")
         dist_columns = held.tile([P, N // P], F32, name="dist_columns")
         offsets = held.tile([P, N // 16], U16, name="offsets")
         x_f32 = [held.tile([P, S], F32, name=f"x_f32_{b}") for b in range(BLOCKS)]
@@ -62,18 +62,30 @@ def tile_pgnn_layer_kernel(tc, x, dist, w1, b1, w2, wh, bh, offs, out):
         nc.vector.memset(scratch[:], 0.0)
         nc.scalar.activation(scratch[:], scratch[:], RELU)
         identity = held.tile([P, P], F32, name="identity")
+        ones = held.tile([P, QUADRANT], F32, name="ones")
+        column_number = held.tile([P, QUADRANT], F32, name="column_number", align_bytes=64)
+        row_number = held.tile([P, QUADRANT], F32, name="row_number", align_bytes=64)
+        nc.gpsimd.memset(identity[:], 0.0)
+        nc.vector.memset(ones[:], 1.0)
+        nc.vector.tensor_tensor_scan(column_number[:], ones[:], ones[:], 0.0, MULT, ADD)
+        nc.vector.transpose(row_number[:], column_number[:])
+        for first in range(0, P, QUADRANT):
+            block = slice(first, first + QUADRANT)
+            nc.vector.tensor_tensor(
+                identity[block, block], column_number[block, :], row_number[block, :], IS_EQUAL
+            )
 
-        nc.gpsimd.memset(dist_rows[:], 0.0)
-        make_identity(nc, identity[:])
-        with nc.allow_non_contiguous_dma(reason="one element to a partition"):
-            nc.sync.dma_start(w1_col[:], w1)
-            nc.sync.dma_start(b1_col[:], b1)
+        nc.gpsimd.memset(dist_rows[QUADRANT : 2 * QUADRANT, :], 0.0)
+        nc.gpsimd.memset(dist_rows[2 * QUADRANT :, :], 0.0)
         nc.sync.dma_start(dist_rows[0 : N // P, :], dist.rearrange("o (q j) -> (o q) j", j=P))
         with nc.allow_non_contiguous_dma(reason="one element to a partition"):
             nc.sync.dma_start(w2_col[:], w2)
+            nc.sync.dma_start(w1_col[:], w1)
+            nc.sync.dma_start(b1_col[:], b1)
         for b in range(BLOCKS):
             nc.sync.dma_start(x_f32[b][:], x[b * P : (b + 1) * P, :])
         nc.sync.dma_start(offsets[:], offs)
+        nc.sync.dma_start(wh_sb[:], wh.rearrange("(k p) m -> p k m", p=P))
         with nc.allow_non_contiguous_dma(reason="one element to a partition"):
             nc.sync.dma_start(bh_col[:], bh)
 
@@ -160,26 +172,27 @@ def tile_pgnn_layer_kernel(tc, x, dist, w1, b1, w2, wh, bh, offs, out):
             width = WIDTHS[k]
             h_here = h[:, STARTS[k] : STARTS[k] + width]
             z_here = z_ps[k][:, 0:width]
-            if k in TENSOR_SUMS:
+            if STARTS[k] < TENSOR_SUMS:
                 h_here = h_here.rearrange("p (a n) -> p n a", a=A)
                 z_here = z_here.rearrange("p (n a) -> p n a", a=A)
             nc.scalar.activation(h_here, z_here, RELU, bias=bh_quarter[:, 0:1], scale=0.25)
 
-        def tensor_sums():
-            mean_ps = psum_mean.tile([P, BANK], F32, name="mean_ps")
-            nodes = BANK // A
-            for i, k in enumerate(TENSOR_SUMS):
-                for a in range(A):
-                    nc.tensor.matmul(
-                        mean_ps[:, i * nodes : (i + 1) * nodes],
-                        identity[:],
-                        h[:, STARTS[k] + a * nodes : STARTS[k] + (a + 1) * nodes],
-                        start=(a == 0),
-                        stop=(a == A - 1),
-                    )
-            taken = slice(STARTS[TENSOR_SUMS[0]] // A, STARTS[TENSOR_SUMS[-1]] // A + nodes)
-            nc.scalar.copy(mean[:, taken], mean_ps[:, 0 : len(TENSOR_SUMS) * nodes])
-            nc.sync.dma_start(out[:, taken], mean[:, taken])
+        mean_ps = psum_mean.tile([P, TENSOR_SUMS // A], F32, name="mean_ps")
+
+        def tensor_sum(k):
+            first, nodes = STARTS[k] // A, WIDTHS[k] // A
+            for a in range(A):
+                nc.tensor.matmul(
+                    mean_ps[:, first : first + nodes],
+                    identity[:],
+                    h[:, STARTS[k] + a * nodes : STARTS[k] + (a + 1) * nodes],
+                    start=(a == 0),
+                    stop=(a == A - 1),
+                )
+
+        def store_tensor_sums():
+            nc.scalar.copy(mean[:, 0 : TENSOR_SUMS // A], mean_ps[:])
+            nc.sync.dma_start(out[:, 0 : TENSOR_SUMS // A], mean[:, 0 : TENSOR_SUMS // A])
 
         def mean_and_store(first, entries):
             nodes = slice(first // A, (first + entries) // A)
@@ -191,8 +204,6 @@ def tile_pgnn_layer_kernel(tc, x, dist, w1, b1, w2, wh, bh, offs, out):
             nc.sync.dma_start(out[:, nodes], mean[:, nodes])
 
         turn_dist()
-        wh_sb = early.tile([P, 2 * BLOCKS, M], BF16, name="wh_sb", tag="early")
-        nc.sync.dma_start(wh_sb[:], wh.rearrange("(k p) m -> p k m", p=P))
         spread_dist(0)
         for k in range(PIECES):
             if k + 1 < PIECES:
@@ -208,7 +219,9 @@ def tile_pgnn_layer_kernel(tc, x, dist, w1, b1, w2, wh, bh, offs, out):
             if t < PIECES:
                 gather(t)
                 project(t)
-            if t - 1 == TENSOR_SUMS[-1]:
-                tensor_sums()
+            if 0 < t and STARTS[t - 1] < TENSOR_SUMS:
+                tensor_sum(t - 1)
+                if STARTS[t - 1] + WIDTHS[t - 1] == TENSOR_SUMS:
+                    store_tensor_sums()
         for first, entries in VECTOR_SUMS:
             mean_and_store(first, entries)

@@ -8,8 +8,10 @@ COPY = mybir.ActivationFunctionType.Copy
 MULT = mybir.AluOpType.mult
 IS_EQUAL = mybir.AluOpType.is_equal
 ADD = mybir.AluOpType.add
+MAX = mybir.AluOpType.max
 
 P = 128
+B2 = 0.25
 QUADRANT = 32
 C = 256
 S = 1024
@@ -23,12 +25,7 @@ WIDTHS = [HALF, HALF] + [BANK] * (N // BANK - 2) + [HALF, HALF]
 STARTS = [sum(WIDTHS[:k]) for k in range(len(WIDTHS))]
 PIECES = len(STARTS)
 TENSOR_SUMS = 3 * BANK
-VECTOR_SUMS = [
-    (3 * BANK, 3 * BANK),
-    (6 * BANK, BANK),
-    (7 * BANK, HALF),
-    (7 * BANK + HALF, HALF),
-]
+SHARED_RELUS = N - 2 * BANK
 
 FLOPS = 2 * M * C * N + 2 * M * C * S + 2 * M * N
 
@@ -39,6 +36,7 @@ def tile_pgnn_layer_kernel(tc, x, dist, w1, b1, w2, wh, bh, offs, out):
         tc.tile_pool(name="held", bufs=1) as held,
         tc.tile_pool(name="work", bufs=3) as work,
         tc.tile_pool(name="last_rounded", bufs=2) as last_rounded,
+        tc.tile_pool(name="shared", bufs=3) as shared,
         tc.tile_pool(name="whole", bufs=PIECES) as whole,
         tc.psum_pool(name="psum_dist", bufs=2) as psum_dist,
         tc.psum_pool(name="psum_d", bufs=2) as psum_d,
@@ -91,13 +89,18 @@ def tile_pgnn_layer_kernel(tc, x, dist, w1, b1, w2, wh, bh, offs, out):
 
         w2_wide = held.tile([P, M], BF16, name="w2_wide")
         nc.vector.tensor_copy(w2_wide[:], w2_col[:, 0:1].to_broadcast([P, M]))
-        bh_quarter = held.tile([P, 1], F32, name="bh_quarter")
-        nc.vector.tensor_scalar_mul(bh_quarter[:], bh_col[:], 0.25)
+        b_quarter = held.tile([P, 1], F32, name="b_quarter")
+        minus_b = held.tile([P, 1], F32, name="minus_b")
+        two_b = held.tile([P, 1], F32, name="two_b")
+        nc.vector.tensor_scalar_mul(b_quarter[:], bh_col[:], 1 / A)
+        nc.vector.tensor_scalar_mul(minus_b[:], bh_col[:], -1 / A)
+        nc.vector.tensor_scalar_mul(two_b[:], bh_col[:], 2 / A)
 
         dist_ps = {}
         d_ps = {}
         d_sb = {}
         msg = {}
+        shared_pairs = {}
         z_ps = {}
 
         def turn_dist():
@@ -127,7 +130,7 @@ def tile_pgnn_layer_kernel(tc, x, dist, w1, b1, w2, wh, bh, offs, out):
         def finish_d(k):
             width = WIDTHS[k]
             d_sb[k] = whole.tile([P, BANK], F32, name="d_sb")
-            nc.scalar.activation(d_sb[k][:, 0:width], d_ps[k][:, 0:width], COPY, bias=0.25)
+            nc.scalar.activation(d_sb[k][:, 0:width], d_ps[k][:, 0:width], COPY, bias=B2 / A, scale=1 / A)
 
         def gather(k):
             width = WIDTHS[k]
@@ -175,7 +178,25 @@ def tile_pgnn_layer_kernel(tc, x, dist, w1, b1, w2, wh, bh, offs, out):
             if STARTS[k] < TENSOR_SUMS:
                 h_here = h_here.rearrange("p (a n) -> p n a", a=A)
                 z_here = z_here.rearrange("p (n a) -> p n a", a=A)
-            nc.scalar.activation(h_here, z_here, RELU, bias=bh_quarter[:, 0:1], scale=0.25)
+            nc.scalar.activation(h_here, z_here, RELU, bias=b_quarter[:, 0:1])
+
+        def relu_shared(k):
+            z = z_ps[k][:, 0 : WIDTHS[k]].rearrange("p (n t a) -> p n t a", t=2, a=2)
+            nodes = WIDTHS[k] // A
+            h_low = shared.tile([P, BANK // A, 2], F32, name="h_low")
+            shared_pairs[k] = shared.tile([P, BANK // A, 2], F32, name="shared_pairs")
+            nc.scalar.activation(h_low[:, 0:nodes, :], z[:, :, 0, :], RELU, bias=b_quarter[:, 0:1])
+            nc.vector.scalar_tensor_tensor(
+                shared_pairs[k][:, 0:nodes, :], z[:, :, 1, :], minus_b[:, 0:1], h_low[:, 0:nodes, :], MAX, ADD
+            )
+
+        def mean_of_shared(k):
+            nodes = slice(STARTS[k] // A, (STARTS[k] + WIDTHS[k]) // A)
+            pairs = shared_pairs[k][:, 0 : WIDTHS[k] // A, :]
+            nc.vector.scalar_tensor_tensor(
+                mean[:, nodes], pairs[:, :, 0], two_b[:, 0:1], pairs[:, :, 1], ADD, ADD
+            )
+            nc.sync.dma_start(out[:, nodes], mean[:, nodes])
 
         mean_ps = psum_mean.tile([P, TENSOR_SUMS // A], F32, name="mean_ps")
 
@@ -197,10 +218,9 @@ def tile_pgnn_layer_kernel(tc, x, dist, w1, b1, w2, wh, bh, offs, out):
         def mean_and_store(first, entries):
             nodes = slice(first // A, (first + entries) // A)
             h_by_node = h[:, first : first + entries].rearrange("p (n a) -> p n a", a=A)
-            pairs = work.tile([P, 3 * BANK // A, 2], F32, name="pairs")
-            pairs_here = pairs[:, 0 : entries // A, :]
-            nc.vector.tensor_tensor(pairs_here, h_by_node[:, :, 0:2], h_by_node[:, :, 2:4], ADD)
-            nc.vector.tensor_tensor(mean[:, nodes], pairs_here[:, :, 0], pairs_here[:, :, 1], ADD)
+            pairs = work.tile([P, entries // A, 2], F32, name="pairs")
+            nc.vector.tensor_tensor(pairs[:], h_by_node[:, :, 0:2], h_by_node[:, :, 2:4], ADD)
+            nc.vector.tensor_tensor(mean[:, nodes], pairs[:, :, 0], pairs[:, :, 1], ADD)
             nc.sync.dma_start(out[:, nodes], mean[:, nodes])
 
         turn_dist()
@@ -211,11 +231,14 @@ def tile_pgnn_layer_kernel(tc, x, dist, w1, b1, w2, wh, bh, offs, out):
             start_d(k)
             finish_d(k)
         for b in range(BLOCKS):
-            nc.vector.tensor_copy(x_bf[b][:], x_f32[b][:])
+            nc.vector.tensor_scalar_mul(x_bf[b][:], x_f32[b][:], 1 / A)
 
         for t in range(PIECES + 1):
             if 0 <= t - 1:
-                relu(t - 1)
+                if STARTS[t - 1] < SHARED_RELUS:
+                    relu(t - 1)
+                else:
+                    relu_shared(t - 1)
             if t < PIECES:
                 gather(t)
                 project(t)
@@ -223,5 +246,7 @@ def tile_pgnn_layer_kernel(tc, x, dist, w1, b1, w2, wh, bh, offs, out):
                 tensor_sum(t - 1)
                 if STARTS[t - 1] + WIDTHS[t - 1] == TENSOR_SUMS:
                     store_tensor_sums()
-        for first, entries in VECTOR_SUMS:
-            mean_and_store(first, entries)
+        mean_and_store(TENSOR_SUMS, SHARED_RELUS - TENSOR_SUMS)
+        for k in range(PIECES):
+            if STARTS[k] >= SHARED_RELUS:
+                mean_of_shared(k)

import concourse.mybir as mybir

F32 = mybir.dt.float32
BF16 = mybir.dt.bfloat16
U16 = mybir.dt.uint16
RELU = mybir.ActivationFunctionType.Relu
COPY = mybir.ActivationFunctionType.Copy
MULT = mybir.AluOpType.mult
IS_EQUAL = mybir.AluOpType.is_equal
ADD = mybir.AluOpType.add
MAX = mybir.AluOpType.max

P = 128
B2 = 0.25
QUADRANT = 32
C = 256
S = 1024
A = 4
N = S * A
M = 128
BLOCKS = C // P
BANK = 512
HALF = BANK // 2
WIDTHS = [HALF, HALF] + [BANK] * (N // BANK - 2) + [HALF, HALF]
STARTS = [sum(WIDTHS[:k]) for k in range(len(WIDTHS))]
PIECES = len(STARTS)
TENSOR_SUMS = 3 * BANK
SHARED_RELUS = N - 2 * BANK

FLOPS = 2 * M * C * N + 2 * M * C * S + 2 * M * N


def tile_pgnn_layer_kernel(tc, x, dist, w1, b1, w2, wh, bh, offs, out):
    nc = tc.nc
    with (
        tc.tile_pool(name="held", bufs=1) as held,
        tc.tile_pool(name="work", bufs=3) as work,
        tc.tile_pool(name="last_rounded", bufs=2) as last_rounded,
        tc.tile_pool(name="shared", bufs=3) as shared,
        tc.tile_pool(name="whole", bufs=PIECES) as whole,
        tc.psum_pool(name="psum_dist", bufs=2) as psum_dist,
        tc.psum_pool(name="psum_d", bufs=2) as psum_d,
        tc.psum_pool(name="psum_z", bufs=3) as psum_z,
        tc.psum_pool(name="psum_mean", bufs=1) as psum_mean,
    ):
        w1_col = held.tile([P, 1], F32, name="w1_col")
        b1_col = held.tile([P, 1], F32, name="b1_col")
        w2_col = held.tile([P, 1], BF16, name="w2_col")
        bh_col = held.tile([P, 1], F32, name="bh_col")
        dist_rows = held.tile([P, P], F32, name="dist_rows")
        wh_sb = held.tile([P, 2 * BLOCKS, M], BF16, name="wh_sb")
        dist_columns = held.tile([P, N // P], F32, name="dist_columns")
        offsets = held.tile([P, N // 16], U16, name="offsets")
        x_f32 = [held.tile([P, S], F32, name=f"x_f32_{b}") for b in range(BLOCKS)]
        x_bf = [held.tile([P, S], BF16, name=f"x_bf_{b}") for b in range(BLOCKS)]
        h = held.tile([P, N], F32, name="h")
        mean = held.tile([P, S], F32, name="mean")

        scratch = held.tile([P, 1], F32, name="scratch")
        nc.vector.memset(scratch[:], 0.0)
        nc.scalar.activation(scratch[:], scratch[:], RELU)
        identity = held.tile([P, P], F32, name="identity")
        ones = held.tile([P, QUADRANT], F32, name="ones")
        column_number = held.tile([P, QUADRANT], F32, name="column_number", align_bytes=64)
        row_number = held.tile([P, QUADRANT], F32, name="row_number", align_bytes=64)
        nc.gpsimd.memset(identity[:], 0.0)
        nc.vector.memset(ones[:], 1.0)
        nc.vector.tensor_tensor_scan(column_number[:], ones[:], ones[:], 0.0, MULT, ADD)
        nc.vector.transpose(row_number[:], column_number[:])
        for first in range(0, P, QUADRANT):
            block = slice(first, first + QUADRANT)
            nc.vector.tensor_tensor(
                identity[block, block], column_number[block, :], row_number[block, :], IS_EQUAL
            )

        nc.gpsimd.memset(dist_rows[QUADRANT : 2 * QUADRANT, :], 0.0)
        nc.gpsimd.memset(dist_rows[2 * QUADRANT :, :], 0.0)
        nc.sync.dma_start(dist_rows[0 : N // P, :], dist.rearrange("o (q j) -> (o q) j", j=P))
        with nc.allow_non_contiguous_dma(reason="one element to a partition"):
            nc.sync.dma_start(w2_col[:], w2)
            nc.sync.dma_start(w1_col[:], w1)
            nc.sync.dma_start(b1_col[:], b1)
        for b in range(BLOCKS):
            nc.sync.dma_start(x_f32[b][:], x[b * P : (b + 1) * P, :])
        nc.sync.dma_start(offsets[:], offs)
        nc.sync.dma_start(wh_sb[:], wh.rearrange("(k p) m -> p k m", p=P))
        with nc.allow_non_contiguous_dma(reason="one element to a partition"):
            nc.sync.dma_start(bh_col[:], bh)

        w2_wide = held.tile([P, M], BF16, name="w2_wide")
        nc.vector.tensor_copy(w2_wide[:], w2_col[:, 0:1].to_broadcast([P, M]))
        b_quarter = held.tile([P, 1], F32, name="b_quarter")
        minus_b = held.tile([P, 1], F32, name="minus_b")
        two_b = held.tile([P, 1], F32, name="two_b")
        nc.vector.tensor_scalar_mul(b_quarter[:], bh_col[:], 1 / A)
        nc.vector.tensor_scalar_mul(minus_b[:], bh_col[:], -1 / A)
        nc.vector.tensor_scalar_mul(two_b[:], bh_col[:], 2 / A)

        dist_ps = {}
        d_ps = {}
        d_sb = {}
        msg = {}
        shared_pairs = {}
        z_ps = {}

        def turn_dist():
            turned = psum_dist.tile([P, BANK], F32, name="dist_ps")
            nc.tensor.transpose(turned[:, 0:P], dist_rows[:], identity[:])
            nc.scalar.copy(dist_columns[:], turned[:, 0 : N // P])

        def spread_dist(k):
            dist_ps[k] = psum_dist.tile([P, BANK], F32, name="dist_ps")
            for j in range(0, WIDTHS[k], P):
                q = (STARTS[k] + j) // P
                nc.tensor.transpose(
                    dist_ps[k][:, j : j + P],
                    dist_columns[:, q : q + 1].to_broadcast([P, P]),
                    identity[:],
                )

        def start_d(k):
            width = WIDTHS[k]
            hid = work.tile([P, BANK], BF16, name="hid")
            nc.scalar.activation(
                hid[:, 0:width], dist_ps[k][:, 0:width], RELU, bias=b1_col[:, 0:1], scale=w1_col[:, 0:1]
            )
            d_ps[k] = psum_d.tile([P, BANK], F32, name="d_ps")
            nc.tensor.matmul(d_ps[k][:, 0:width], w2_wide[:], hid[:, 0:width], start=True, stop=True)

        def finish_d(k):
            width = WIDTHS[k]
            d_sb[k] = whole.tile([P, BANK], F32, name="d_sb")
            nc.scalar.activation(d_sb[k][:, 0:width], d_ps[k][:, 0:width], COPY, bias=B2 / A, scale=1 / A)

        def gather(k):
            width = WIDTHS[k]
            piece_offsets = offsets[:, STARTS[k] // 16 : (STARTS[k] + width) // 16]
            msg[k] = [whole.tile([P, BANK], F32, name=f"msg{b}") for b in range(BLOCKS)]
            for b in range(BLOCKS):
                nc.vector.tensor_tensor(
                    msg[k][b][:, 0:width], x_f32[b][:].indirect(piece_offsets), d_sb[k][:, 0:width], MULT
                )

        def project(k):
            width = WIDTHS[k]
            last_bank = STARTS[k] >= N - BANK
            rounded = last_rounded if last_bank else work
            msg_bf = [rounded.tile([P, BANK], BF16, name=f"msg_bf{b}") for b in range(BLOCKS)]
            for b in range(BLOCKS):
                if last_bank:
                    nc.vector.tensor_copy(msg_bf[b][:, 0:width], msg[k][b][:, 0:width])
                else:
                    nc.scalar.activation(msg_bf[b][:, 0:width], msg[k][b][:, 0:width], COPY)
            z_ps[k] = psum_z.tile([P, BANK], F32, name="z_ps")
            z_by_node = z_ps[k][:, 0:width].rearrange("p (n a) -> p n a", a=A)
            for b in range(BLOCKS):
                own = x_bf[b][:, STARTS[k] // A : (STARTS[k] + width) // A]
                nc.tensor.matmul(
                    z_by_node,
                    wh_sb[:, BLOCKS + b, :],
                    own.unsqueeze(2).to_broadcast([P, width // A, A]),
                    start=(b == 0),
                    stop=False,
                )
            for b in range(BLOCKS):
                nc.tensor.matmul(
                    z_ps[k][:, 0:width],
                    wh_sb[:, b, :],
                    msg_bf[b][:, 0:width],
                    start=False,
                    stop=(b == BLOCKS - 1),
                )

        def relu(k):
            width = WIDTHS[k]
            h_here = h[:, STARTS[k] : STARTS[k] + width]
            z_here = z_ps[k][:, 0:width]
            if STARTS[k] < TENSOR_SUMS:
                h_here = h_here.rearrange("p (a n) -> p n a", a=A)
                z_here = z_here.rearrange("p (n a) -> p n a", a=A)
            nc.scalar.activation(h_here, z_here, RELU, bias=b_quarter[:, 0:1])

        def relu_shared(k):
            z = z_ps[k][:, 0 : WIDTHS[k]].rearrange("p (n t a) -> p n t a", t=2, a=2)
            nodes = WIDTHS[k] // A
            h_low = shared.tile([P, BANK // A, 2], F32, name="h_low")
            shared_pairs[k] = shared.tile([P, BANK // A, 2], F32, name="shared_pairs")
            nc.scalar.activation(h_low[:, 0:nodes, :], z[:, :, 0, :], RELU, bias=b_quarter[:, 0:1])
            nc.vector.scalar_tensor_tensor(
                shared_pairs[k][:, 0:nodes, :], z[:, :, 1, :], minus_b[:, 0:1], h_low[:, 0:nodes, :], MAX, ADD
            )

        def mean_of_shared(k):
            nodes = slice(STARTS[k] // A, (STARTS[k] + WIDTHS[k]) // A)
            pairs = shared_pairs[k][:, 0 : WIDTHS[k] // A, :]
            nc.vector.scalar_tensor_tensor(
                mean[:, nodes], pairs[:, :, 0], two_b[:, 0:1], pairs[:, :, 1], ADD, ADD
            )
            nc.sync.dma_start(out[:, nodes], mean[:, nodes])

        mean_ps = psum_mean.tile([P, TENSOR_SUMS // A], F32, name="mean_ps")

        def tensor_sum(k):
            first, nodes = STARTS[k] // A, WIDTHS[k] // A
            for a in range(A):
                nc.tensor.matmul(
                    mean_ps[:, first : first + nodes],
                    identity[:],
                    h[:, STARTS[k] + a * nodes : STARTS[k] + (a + 1) * nodes],
                    start=(a == 0),
                    stop=(a == A - 1),
                )

        def store_tensor_sums():
            nc.scalar.copy(mean[:, 0 : TENSOR_SUMS // A], mean_ps[:])
            nc.sync.dma_start(out[:, 0 : TENSOR_SUMS // A], mean[:, 0 : TENSOR_SUMS // A])

        def mean_and_store(first, entries):
            nodes = slice(first // A, (first + entries) // A)
            h_by_node = h[:, first : first + entries].rearrange("p (n a) -> p n a", a=A)
            pairs = work.tile([P, entries // A, 2], F32, name="pairs")
            nc.vector.tensor_tensor(pairs[:], h_by_node[:, :, 0:2], h_by_node[:, :, 2:4], ADD)
            nc.vector.tensor_tensor(mean[:, nodes], pairs[:, :, 0], pairs[:, :, 1], ADD)
            nc.sync.dma_start(out[:, nodes], mean[:, nodes])

        turn_dist()
        spread_dist(0)
        for k in range(PIECES):
            if k + 1 < PIECES:
                spread_dist(k + 1)
            start_d(k)
            finish_d(k)
        for b in range(BLOCKS):
            nc.vector.tensor_scalar_mul(x_bf[b][:], x_f32[b][:], 1 / A)

        for t in range(PIECES + 1):
            if 0 <= t - 1:
                if STARTS[t - 1] < SHARED_RELUS:
                    relu(t - 1)
                else:
                    relu_shared(t - 1)
            if t < PIECES:
                gather(t)
                project(t)
            if 0 < t and STARTS[t - 1] < TENSOR_SUMS:
                tensor_sum(t - 1)
                if STARTS[t - 1] + WIDTHS[t - 1] == TENSOR_SUMS:
                    store_tensor_sums()
        mean_and_store(TENSOR_SUMS, SHARED_RELUS - TENSOR_SUMS)
        for k in range(PIECES):
            if STARTS[k] >= SHARED_RELUS:
                mean_of_shared(k)
